import numpy as np
import ml_dtypes


def mxq(x, axis, fmt="e4m3"):
    dtype, down = {"e4m3": (ml_dtypes.float8_e4m3fn, 7), "e5m2": (ml_dtypes.float8_e5m2, 14)}[fmt]
    v = np.moveaxis(np.asarray(x, np.float32).astype(ml_dtypes.bfloat16).astype(np.float64), axis, -1)
    blocks = v.reshape(v.shape[:-1] + (-1, 32))
    amax = np.abs(blocks).max(-1, keepdims=True)
    byte = np.maximum(np.where(amax > 0, np.frexp(amax)[1] - 1 + 127, 0) - down, 1)
    scale = np.exp2(byte - 127.0)
    codes = (blocks / scale).astype(np.float32).astype(dtype).astype(np.float64)
    return np.moveaxis((codes * scale).reshape(v.shape), -1, axis)


WIDE = False


def mx_kscale(k):
    if not WIDE:
        return np.ones(k)
    levels = np.array([10, -10, 5, -5, 0])
    a = np.random.permutation(np.resize(levels, k // 512 * 4)).reshape(k // 512, 4)
    idx = np.arange(k)
    return np.exp2(a[idx // 512, idx % 128 // 32])


BF16 = ml_dtypes.bfloat16


def bf(x):
    return np.asarray(x, np.float32).astype(BF16)


def f64(x):
    return np.asarray(x).astype(np.float64)


E2M1 = np.array([0.0, 0.5, 1.0, 1.5, 2.0, 3.0, 4.0, 6.0, -0.0, -0.5, -1.0, -1.5, -2.0, -3.0, -4.0, -6.0])


def pack_weight(w, fmt):
    k, n = w.shape
    w = f64(bf(w)).reshape(k // 32, 32, n)
    amax = np.abs(w).max(1)
    if fmt == "e4m3":
        byte = np.frexp(amax)[1] - 1 + 127 - 7
    else:
        mant, ex = np.frexp(amax / 6.0)
        byte = np.where(mant > 0.5, ex, ex - 1) + 127
    byte = np.clip(np.where(amax > 0, byte, 1), 1, 254)
    scaled = (w * np.exp2(127.0 - byte)[:, None, :]).reshape(k, n).astype(np.float32)
    by_word = np.ascontiguousarray(scaled.reshape(k // 512, 128, 4, n).transpose(0, 1, 3, 2))
    if fmt == "e4m3":
        words = by_word.astype(ml_dtypes.float8_e4m3fn).view(np.uint8)
    else:
        c = by_word.astype(ml_dtypes.float4_e2m1fn).view(np.uint8) & 0xF
        words = c[..., 0::2] | (c[..., 1::2] << 4)
    return np.ascontiguousarray(words), np.ascontiguousarray(byte.astype(np.uint8).reshape(k // 512, 16, n))


def unpack_weight(words, scales, fmt):
    g, p, n, _ = words.shape
    if fmt == "e4m3":
        vals = np.ascontiguousarray(words).view(ml_dtypes.float8_e4m3fn).astype(np.float64)
    else:
        nib = np.empty((g, p, n, 4), np.uint8)
        nib[..., 0::2] = words & 0xF
        nib[..., 1::2] = words >> 4
        vals = E2M1[nib]
    vals = vals * np.repeat(np.exp2(scales.astype(np.float64) - 127.0), 8, axis=1)[..., None]
    return vals.transpose(0, 1, 3, 2).reshape(g * 512, n)


B, N, SIZE, CH = 256, 16, 1024, 512


def sigmoid(v):
    return 1.0 / (1.0 + np.exp(-v))


def setup_inputs():
    s = mx_kscale(SIZE)
    d = {"z0": bf(np.random.standard_normal((B, SIZE)) * s),
         "h_tilde": bf(np.random.standard_normal((B, CH)) * np.sqrt(N)),
         "fc_sum": bf(np.random.standard_normal((B, CH)) * 1.2)}
    for g in ("i", "o", "u"):
        words, scales = pack_weight((np.random.standard_normal((CH, SIZE)) / np.sqrt(SIZE) / s).T, "e4m3")
        d["W_" + g + "_words"] = words
        d["W_" + g + "_scales"] = scales
        d["U_" + g] = bf(np.random.standard_normal((CH, CH)) / np.sqrt(CH * N))
        d["b_" + g] = bf(np.random.standard_normal(CH) * 0.5)
    return d


def reference(z0, h_tilde, fc_sum, W_i_words, W_i_scales, U_i, b_i, W_o_words, W_o_scales, U_o, b_o, W_u_words, W_u_scales, U_u, b_u):
    zq = mxq(f64(z0), 1, "e4m3")
    ht = f64(h_tilde)
    i_j = sigmoid((zq @ unpack_weight(W_i_words, W_i_scales, "e4m3")) + ht @ f64(U_i).T + f64(b_i))
    o_j = sigmoid((zq @ unpack_weight(W_o_words, W_o_scales, "e4m3")) + ht @ f64(U_o).T + f64(b_o))
    u_j = np.tanh((zq @ unpack_weight(W_u_words, W_u_scales, "e4m3")) + ht @ f64(U_u).T + f64(b_u))
    c_j = i_j * u_j + f64(fc_sum)
    h_j = o_j * np.tanh(c_j)
    return np.concatenate([h_j, c_j], axis=-1)

@@ -1,0 +1,259 @@
+from contextlib import ExitStack
+
+import concourse.mybir as mybir
+from concourse.masks import make_identity
+
+F32 = mybir.dt.float32
+BF16 = mybir.dt.bfloat16
+I32 = mybir.dt.int32
+U32 = mybir.dt.uint32
+U8 = mybir.dt.uint8
+FP8X4 = mybir.dt.float8_e4m3fn_x4
+ADD = mybir.AluOpType.add
+MULT = mybir.AluOpType.mult
+SIGMOID = mybir.ActivationFunctionType.Sigmoid
+TANH = mybir.ActivationFunctionType.Tanh
+
+P = 128
+ROW_TILES = 2
+SIZE = 1024
+CH = 512
+PASSES = SIZE // (4 * P)
+HALVES = CH // (2 * P)
+BANK = 512
+GATES = ("u", "i", "o")
+
+FLOPS = 2 * 256 * (3 * CH) * (SIZE + CH)
+
+
+def tile_treelstm_pb_kernel(
+    tc,
+    z0,
+    h_tilde,
+    fc_sum,
+    W_i_words,
+    W_i_scales,
+    U_i,
+    b_i,
+    W_o_words,
+    W_o_scales,
+    U_o,
+    b_o,
+    W_u_words,
+    W_u_scales,
+    U_u,
+    b_u,
+    out,
+):
+    nc = tc.nc
+    words_in = {"u": W_u_words, "i": W_i_words, "o": W_o_words}
+    scales_in = {"u": W_u_scales, "i": W_i_scales, "o": W_o_scales}
+    U_in = {"u": U_u, "i": U_i, "o": U_o}
+    b_in = {"u": b_u, "i": b_i, "o": b_o}
+    func = {"u": TANH, "i": SIGMOID, "o": SIGMOID}
+    column = {"u": 0, "i": 1, "o": 2}
+
+    with ExitStack() as ctx:
+        keep = ctx.enter_context(tc.tile_pool(name="keep", bufs=1))
+        psum = ctx.enter_context(tc.psum_pool(name="psum", bufs=8))
+        ctx.enter_context(tc.manual_schedule())
+
+        bias_rows = keep.tile([P, 3, CH], BF16, name="bias_rows")
+        nc.vector.memset(bias_rows[:].bitcast(I32), 0)
+        warm_in = keep.tile([P, 1], F32, name="warm_in")
+        warm_out = keep.tile([P, 1], F32, name="warm_out")
+        nc.vector.memset(warm_in[:], 0.0)
+        ones = keep.tile([P, P], BF16, name="ones")
+        nc.vector.memset(ones[:], 1.0)
+        w_planes = keep.tile([P, 3, CH], U8, name="w_planes", align_bytes=64)
+        nc.vector.memset(w_planes[:].bitcast(I32), 0)
+        ident = keep.tile([P, P], F32, name="ident")
+        make_identity(nc, ident[:])
+
+        ht_sb = keep.tile([P, ROW_TILES, CH], BF16, name="ht_sb")
+        z_sb = keep.tile([P, ROW_TILES, SIZE], BF16, name="z_sb")
+        fc_sb = keep.tile([P, ROW_TILES, CH], BF16, name="fc_sb")
+        U_sb = {}
+        w_words = {}
+        for x in GATES:
+            U_sb[x] = keep.tile([P, 4, CH], BF16, name="U_sb_" + x)
+            w_words[x] = keep.tile([P, PASSES, 4 * CH], U8, name="w_words_" + x, align_bytes=64)
+
+        def load_U(x):
+            nc.sync.dma_start(out=U_sb[x][:], in_=U_in[x].rearrange("(p t) k -> p t k", t=4))
+
+        def load_scales(x):
+            for quadrant in range(4):
+                nc.sync.dma_start(
+                    out=w_planes[32 * quadrant : 32 * quadrant + 4 * PASSES, column[x], :].bitcast(I32),
+                    in_=scales_in[x][:, 4 * quadrant : 4 * quadrant + 4, :].bitcast(I32),
+                )
+
+        def load_words(x):
+            nc.sync.dma_start(
+                out=w_words[x][:].bitcast(I32),
+                in_=words_in[x].rearrange("g p n t -> p g (n t)").bitcast(I32),
+            )
+
+        nc.sync.dma_start(out=ht_sb[:], in_=h_tilde.rearrange("(p j) k -> p j k", j=ROW_TILES))
+        load_U("u")
+        load_U("i")
+        nc.sync.dma_start(out=z_sb[:], in_=z0.rearrange("(p j) k -> p j k", j=ROW_TILES))
+        load_U("o")
+        for x in GATES:
+            load_scales(x)
+        load_words("u")
+        load_words("i")
+        nc.sync.dma_start(out=fc_sb[:], in_=fc_sum.rearrange("(p j) k -> p j k", j=ROW_TILES))
+        load_words("o")
+        for x in GATES:
+            nc.scalar.dma_start(
+                out=bias_rows[0:1, column[x], :], in_=b_in[x].rearrange("(o n) -> o n", o=1)
+            )
+        nc.scalar.activation(out=warm_out[:], in_=warm_in[:], func=SIGMOID)
+
+        htT = keep.tile([P, ROW_TILES, HALVES, 2, P], BF16, name="htT")
+        UT = {}
+        for x in GATES:
+            UT[x] = keep.tile([P, HALVES, 2 * CH], BF16, name="UT_" + x)
+        bias_bc = keep.tile([P, 3, CH], F32, name="bias_bc")
+        z_grouped = keep.tile([P, ROW_TILES, PASSES * P * 4], BF16, name="z_grouped", align_bytes=64)
+        z_codes = keep.tile([P, ROW_TILES, PASSES * P], U32, name="z_codes", align_bytes=64)
+        z_scales = keep.tile([P, ROW_TILES, PASSES * P], U8, name="z_scales", align_bytes=64)
+        partial = {}
+        gate = {}
+        for j in range(ROW_TILES):
+            for x in GATES:
+                partial[(j, x)] = keep.tile([P, CH], F32, name="partial_%d_%s" % (j, x))
+                gate[(j, x)] = keep.tile([P, CH], F32, name="gate_%d_%s" % (j, x))
+        iu = [keep.tile([P, CH], F32, name="iu_%d" % j) for j in range(ROW_TILES)]
+        tanh_c = [keep.tile([P, CH], F32, name="tanh_c_%d" % j) for j in range(ROW_TILES)]
+        result = [keep.tile([P, 2 * CH], F32, name="result_%d" % j) for j in range(ROW_TILES)]
+        out_rows = out.rearrange("(p j) n -> p j n", j=ROW_TILES)
+
+        def new_bank():
+            bank = psum.tile([P, BANK], F32, name="bank")
+            return bank
+
+        def transpose_ht():
+            bank = new_bank()
+            ht_words = ht_sb[:].bitcast(F32)
+            for j in range(ROW_TILES):
+                for u in range(HALVES):
+                    a = j * HALVES + u
+                    nc.tensor.transpose(
+                        out=bank[:, a * P : (a + 1) * P],
+                        in_=ht_words[:, j, u * P : (u + 1) * P],
+                        identity=ident[:],
+                    )
+            nc.vector.tensor_copy(
+                out=htT[:].rearrange("q j u e p -> q (j u) e p"),
+                in_=bank[:].bitcast(BF16).rearrange("q (a p e) -> q a e p", a=ROW_TILES * HALVES, e=2),
+            )
+
+        def prepare_gate(x):
+            U_words = U_sb[x][:].bitcast(F32)
+            for u in range(HALVES):
+                bank = new_bank()
+                for t in range(4):
+                    nc.tensor.transpose(
+                        out=bank[:, t * P : (t + 1) * P],
+                        in_=U_words[:, t, u * P : (u + 1) * P],
+                        identity=ident[:],
+                    )
+                copy = nc.scalar.copy if u == 0 else nc.vector.tensor_copy
+                copy(
+                    out=UT[x][:, u, :].bitcast(F32).rearrange("q (p t) -> q p t", t=4),
+                    in_=bank[:].rearrange("q (t p) -> q p t", t=4),
+                )
+            bank = new_bank()
+            nc.tensor.matmul(out=bank[:], lhsT=ones[:], rhs=bias_rows[:, column[x], :], start=True, stop=True)
+            nc.scalar.copy(out=bias_bc[:, column[x], :], in_=bank[:])
+
+        def transpose_z(j):
+            bank = new_bank()
+            z_words = z_sb[:].bitcast(F32)
+            for g in range(PASSES):
+                for u in range(2):
+                    a = 2 * g + u
+                    nc.tensor.transpose(
+                        out=bank[:, a * P : (a + 1) * P],
+                        in_=z_words[:, j, 256 * g + u : 256 * (g + 1) : 2],
+                        identity=ident[:],
+                    )
+            copy = nc.scalar.copy if j == 0 else nc.vector.tensor_copy
+            copy(
+                out=z_grouped[:, j, :].bitcast(F32).rearrange("q (g b u) -> q g b u", g=PASSES, u=2),
+                in_=bank[:].rearrange("q (g u b) -> q g b u", g=PASSES, u=2),
+            )
+
+        def quantise_z(j):
+            nc.vector.quantize_mx(
+                out=z_codes[:, j, :].bitcast(FP8X4), scales=z_scales[:, j, :], in_=z_grouped[:, j, :]
+            )
+
+        def plain_product(j, x):
+            acc = new_bank()
+            UT_pairs = UT[x][:].rearrange("q u (n e) -> q u n e", e=2)
+            for u in range(HALVES):
+                for e in range(2):
+                    nc.tensor.matmul(
+                        out=acc[:],
+                        lhsT=htT[:, j, u, e, :],
+                        rhs=UT_pairs[:, u, :, e],
+                        start=(u == 0 and e == 0),
+                        stop=(u == HALVES - 1 and e == 1),
+                    )
+            nc.vector.tensor_tensor(
+                out=partial[(j, x)][:], in0=acc[:], in1=bias_bc[:, column[x], :], op=ADD
+            )
+
+        def mx_product(j, x):
+            acc = new_bank()
+            for g in range(PASSES):
+                nc.tensor.matmul_mx(
+                    out=acc[:],
+                    lhsT=z_codes[:, j, g * P : (g + 1) * P].bitcast(FP8X4),
+                    lhsT_scale=z_scales[:, j, g * P : (g + 1) * P],
+                    rhs=w_words[x][:, g, :].bitcast(FP8X4),
+                    rhs_scale=w_planes[4 * g : P, column[x], :],
+                    start=(g == 0),
+                    stop=(g == PASSES - 1),
+                )
+            nc.vector.tensor_tensor(out=partial[(j, x)][:], in0=acc[:], in1=partial[(j, x)][:], op=ADD)
+            nc.scalar.activation(out=gate[(j, x)][:], in_=partial[(j, x)][:], func=func[x])
+
+        def cell(j, engine):
+            engine.tensor_tensor(out=iu[j][:], in0=gate[(j, "i")][:], in1=gate[(j, "u")][:], op=MULT)
+            engine.tensor_tensor(out=result[j][:, CH:], in0=iu[j][:], in1=fc_sb[:, j, :], op=ADD)
+            nc.sync.dma_start(out=out_rows[:, j, CH:], in_=result[j][:, CH:])
+            nc.scalar.activation(out=tanh_c[j][:], in_=result[j][:, CH:], func=TANH)
+
+        def hidden(j, engine):
+            engine.tensor_tensor(out=result[j][:, :CH], in0=gate[(j, "o")][:], in1=tanh_c[j][:], op=MULT)
+            nc.sync.dma_start(out=out_rows[:, j, :CH], in_=result[j][:, :CH])
+
+        transpose_ht()
+        prepare_gate("u")
+        prepare_gate("i")
+        plain_product(0, "u")
+        plain_product(1, "u")
+        transpose_z(0)
+        transpose_z(1)
+        quantise_z(0)
+        quantise_z(1)
+        plain_product(0, "i")
+        plain_product(1, "i")
+        prepare_gate("o")
+        mx_product(0, "u")
+        mx_product(0, "i")
+        mx_product(1, "u")
+        mx_product(1, "i")
+        cell(0, nc.gpsimd)
+        plain_product(0, "o")
+        plain_product(1, "o")
+        cell(1, nc.vector)
+        mx_product(0, "o")
+        hidden(0, nc.gpsimd)
+        mx_product(1, "o")
+        hidden(1, nc.vector)

@@ -95,22 +95,25 @@ def tile_treelstm_pb_kernel(
                 in_=words_in[x].rearrange("g p n t -> p g (n t)").bitcast(I32),
             )
 
-        nc.sync.dma_start(out=ht_sb[:], in_=h_tilde.rearrange("(p j) k -> p j k", j=ROW_TILES))
-        load_U("u")
-        load_U("i")
-        nc.sync.dma_start(out=z_sb[:], in_=z0.rearrange("(p j) k -> p j k", j=ROW_TILES))
-        load_U("o")
-        for x in GATES:
-            load_scales(x)
-        load_words("u")
-        load_words("i")
-        nc.sync.dma_start(out=fc_sb[:], in_=fc_sum.rearrange("(p j) k -> p j k", j=ROW_TILES))
-        load_words("o")
+        bias_in = keep.tile([1, 3, CH], BF16, name="bias_in")
         for x in GATES:
             nc.scalar.dma_start(
-                out=bias_rows[0:1, column[x], :], in_=b_in[x].rearrange("(o n) -> o n", o=1)
+                out=bias_in[0:1, column[x], :], in_=b_in[x].rearrange("(o n) -> o n", o=1)
             )
+        nc.vector.tensor_copy(out=bias_rows[0:1, :, :], in_=bias_in[:])
         nc.scalar.activation(out=warm_out[:], in_=warm_in[:], func=SIGMOID)
+        nc.sync.dma_start(out=ht_sb[:], in_=h_tilde.rearrange("(p j) k -> p j k", j=ROW_TILES))
+        load_U("u")
+        nc.sync.dma_start(out=z_sb[:], in_=z0.rearrange("(p j) k -> p j k", j=ROW_TILES))
+        load_U("i")
+        load_scales("u")
+        load_words("u")
+        load_words("i")
+        load_U("o")
+        load_scales("i")
+        nc.sync.dma_start(out=fc_sb[:], in_=fc_sum.rearrange("(p j) k -> p j k", j=ROW_TILES))
+        load_words("o")
+        load_scales("o")
 
         htT = keep.tile([P, ROW_TILES, HALVES, 2, P], BF16, name="htT")
         UT = {}
@@ -151,7 +154,12 @@ def tile_treelstm_pb_kernel(
                 in_=bank[:].bitcast(BF16).rearrange("q (a p e) -> q a e p", a=ROW_TILES * HALVES, e=2),
             )
 
-        def prepare_gate(x):
+        def broadcast_bias(x):
+            bank = new_bank()
+            nc.tensor.matmul(out=bank[:], lhsT=ones[:], rhs=bias_rows[:, column[x], :], start=True, stop=True)
+            nc.scalar.copy(out=bias_bc[:, column[x], :], in_=bank[:])
+
+        def transpose_U(x, copies):
             U_words = U_sb[x][:].bitcast(F32)
             for u in range(HALVES):
                 bank = new_bank()
@@ -161,16 +169,12 @@ def tile_treelstm_pb_kernel(
                         in_=U_words[:, t, u * P : (u + 1) * P],
                         identity=ident[:],
                     )
-                copy = nc.scalar.copy if u == 0 else nc.vector.tensor_copy
-                copy(
+                copies[u](
                     out=UT[x][:, u, :].bitcast(F32).rearrange("q (p t) -> q p t", t=4),
                     in_=bank[:].rearrange("q (t p) -> q p t", t=4),
                 )
-            bank = new_bank()
-            nc.tensor.matmul(out=bank[:], lhsT=ones[:], rhs=bias_rows[:, column[x], :], start=True, stop=True)
-            nc.scalar.copy(out=bias_bc[:, column[x], :], in_=bank[:])
 
-        def transpose_z(j):
+        def transpose_z(j, copy):
             bank = new_bank()
             z_words = z_sb[:].bitcast(F32)
             for g in range(PASSES):
@@ -181,7 +185,6 @@ def tile_treelstm_pb_kernel(
                         in_=z_words[:, j, 256 * g + u : 256 * (g + 1) : 2],
                         identity=ident[:],
                     )
-            copy = nc.scalar.copy if j == 0 else nc.vector.tensor_copy
             copy(
                 out=z_grouped[:, j, :].bitcast(F32).rearrange("q (g b u) -> q g b u", g=PASSES, u=2),
                 in_=bank[:].rearrange("q (g u b) -> q g b u", g=PASSES, u=2),
@@ -194,6 +197,11 @@ def tile_treelstm_pb_kernel(
 
         def plain_product(j, x):
             acc = new_bank()
+            bias_in_group = x == "o"
+            if bias_in_group:
+                nc.tensor.matmul(
+                    out=acc[:], lhsT=ones[:], rhs=bias_rows[:, column[x], :], start=True, stop=False
+                )
             UT_pairs = UT[x][:].rearrange("q u (n e) -> q u n e", e=2)
             for u in range(HALVES):
                 for e in range(2):
@@ -201,12 +209,17 @@ def tile_treelstm_pb_kernel(
                         out=acc[:],
                         lhsT=htT[:, j, u, e, :],
                         rhs=UT_pairs[:, u, :, e],
-                        start=(u == 0 and e == 0),
+                        start=(u == 0 and e == 0 and not bias_in_group),
                         stop=(u == HALVES - 1 and e == 1),
                     )
-            nc.vector.tensor_tensor(
-                out=partial[(j, x)][:], in0=acc[:], in1=bias_bc[:, column[x], :], op=ADD
-            )
+            if not bias_in_group:
+                nc.vector.tensor_tensor(
+                    out=partial[(j, x)][:], in0=acc[:], in1=bias_bc[:, column[x], :], op=ADD
+                )
+            elif j == 0:
+                nc.scalar.copy(out=partial[(j, x)][:], in_=acc[:])
+            else:
+                nc.vector.tensor_copy(out=partial[(j, x)][:], in_=acc[:])
 
         def mx_product(j, x):
             acc = new_bank()
@@ -223,37 +236,39 @@ def tile_treelstm_pb_kernel(
             nc.vector.tensor_tensor(out=partial[(j, x)][:], in0=acc[:], in1=partial[(j, x)][:], op=ADD)
             nc.scalar.activation(out=gate[(j, x)][:], in_=partial[(j, x)][:], func=func[x])
 
-        def cell(j, engine):
+        def cell_state(j, engine):
             engine.tensor_tensor(out=iu[j][:], in0=gate[(j, "i")][:], in1=gate[(j, "u")][:], op=MULT)
             engine.tensor_tensor(out=result[j][:, CH:], in0=iu[j][:], in1=fc_sb[:, j, :], op=ADD)
             nc.sync.dma_start(out=out_rows[:, j, CH:], in_=result[j][:, CH:])
+
+        def tanh_cell(j):
             nc.scalar.activation(out=tanh_c[j][:], in_=result[j][:, CH:], func=TANH)
 
-        def hidden(j, engine):
-            engine.tensor_tensor(out=result[j][:, :CH], in0=gate[(j, "o")][:], in1=tanh_c[j][:], op=MULT)
+        def hidden(j):
+            nc.vector.tensor_tensor(out=result[j][:, :CH], in0=gate[(j, "o")][:], in1=tanh_c[j][:], op=MULT)
             nc.sync.dma_start(out=out_rows[:, j, :CH], in_=result[j][:, :CH])
 
+        broadcast_bias("u")
+        broadcast_bias("i")
         transpose_ht()
-        prepare_gate("u")
-        prepare_gate("i")
-        plain_product(0, "u")
-        plain_product(1, "u")
-        transpose_z(0)
-        transpose_z(1)
+        transpose_U("u", (nc.scalar.copy, nc.vector.tensor_copy))
+        transpose_z(0, nc.scalar.copy)
+        transpose_z(1, nc.vector.tensor_copy)
         quantise_z(0)
         quantise_z(1)
-        plain_product(0, "i")
-        plain_product(1, "i")
-        prepare_gate("o")
-        mx_product(0, "u")
-        mx_product(0, "i")
-        mx_product(1, "u")
-        mx_product(1, "i")
-        cell(0, nc.gpsimd)
+        for x, following in (("u", "i"), ("i", "o")):
+            plain_product(0, x)
+            transpose_U(following, (nc.scalar.copy, nc.scalar.copy))
+            plain_product(1, x)
+            mx_product(0, x)
+            mx_product(1, x)
+        cell_state(0, nc.gpsimd)
         plain_product(0, "o")
+        cell_state(1, nc.vector)
+        tanh_cell(1)
         plain_product(1, "o")
-        cell(1, nc.vector)
+        tanh_cell(0)
         mx_product(0, "o")
-        hidden(0, nc.gpsimd)
         mx_product(1, "o")
-        hidden(1, nc.vector)
+        hidden(0)
+        hidden(1)

@@ -96,13 +96,13 @@ def tile_treelstm_pb_kernel(
             )
 
         bias_in = keep.tile([1, 3, CH], BF16, name="bias_in")
+        nc.sync.dma_start(out=ht_sb[:], in_=h_tilde.rearrange("(p j) k -> p j k", j=ROW_TILES))
         for x in GATES:
-            nc.scalar.dma_start(
+            nc.sync.dma_start(
                 out=bias_in[0:1, column[x], :], in_=b_in[x].rearrange("(o n) -> o n", o=1)
             )
         nc.vector.tensor_copy(out=bias_rows[0:1, :, :], in_=bias_in[:])
         nc.scalar.activation(out=warm_out[:], in_=warm_in[:], func=SIGMOID)
-        nc.sync.dma_start(out=ht_sb[:], in_=h_tilde.rearrange("(p j) k -> p j k", j=ROW_TILES))
         load_U("u")
         nc.sync.dma_start(out=z_sb[:], in_=z0.rearrange("(p j) k -> p j k", j=ROW_TILES))
         load_U("i")
@@ -248,16 +248,17 @@ def tile_treelstm_pb_kernel(
             nc.vector.tensor_tensor(out=result[j][:, :CH], in0=gate[(j, "o")][:], in1=tanh_c[j][:], op=MULT)
             nc.sync.dma_start(out=out_rows[:, j, :CH], in_=result[j][:, :CH])
 
+        transpose_ht()
         broadcast_bias("u")
         broadcast_bias("i")
-        transpose_ht()
         transpose_U("u", (nc.scalar.copy, nc.vector.tensor_copy))
         transpose_z(0, nc.scalar.copy)
-        transpose_z(1, nc.vector.tensor_copy)
         quantise_z(0)
-        quantise_z(1)
         for x, following in (("u", "i"), ("i", "o")):
             plain_product(0, x)
+            if x == "u":
+                transpose_z(1, nc.scalar.copy)
+                quantise_z(1)
             transpose_U(following, (nc.scalar.copy, nc.scalar.copy))
             plain_product(1, x)
             mx_product(0, x)

@@ -56,7 +56,6 @@ def tile_treelstm_pb_kernel(
     with ExitStack() as ctx:
         keep = ctx.enter_context(tc.tile_pool(name="keep", bufs=1))
         psum = ctx.enter_context(tc.psum_pool(name="psum", bufs=8))
-        ctx.enter_context(tc.manual_schedule())
 
         bias_rows = keep.tile([P, 3, CH], BF16, name="bias_rows")
         nc.vector.memset(bias_rows[:].bitcast(I32), 0)

@@ -56,6 +56,7 @@ def tile_treelstm_pb_kernel(
     with ExitStack() as ctx:
         keep = ctx.enter_context(tc.tile_pool(name="keep", bufs=1))
         psum = ctx.enter_context(tc.psum_pool(name="psum", bufs=8))
+        ctx.enter_context(tc.manual_schedule())
 
         bias_rows = keep.tile([P, 3, CH], BF16, name="bias_rows")
         nc.vector.memset(bias_rows[:].bitcast(I32), 0)
@@ -103,16 +104,16 @@ def tile_treelstm_pb_kernel(
         nc.vector.tensor_copy(out=bias_rows[0:1, :, :], in_=bias_in[:])
         nc.scalar.activation(out=warm_out[:], in_=warm_in[:], func=SIGMOID)
         load_U("u")
-        nc.sync.dma_start(out=z_sb[:], in_=z0.rearrange("(p j) k -> p j k", j=ROW_TILES))
         load_U("i")
+        nc.sync.dma_start(out=z_sb[:], in_=z0.rearrange("(p j) k -> p j k", j=ROW_TILES))
         load_scales("u")
         load_words("u")
+        load_scales("i")
         load_words("i")
         load_U("o")
-        load_scales("i")
-        nc.sync.dma_start(out=fc_sb[:], in_=fc_sum.rearrange("(p j) k -> p j k", j=ROW_TILES))
-        load_words("o")
         load_scales("o")
+        load_words("o")
+        nc.sync.dma_start(out=fc_sb[:], in_=fc_sum.rearrange("(p j) k -> p j k", j=ROW_TILES))
 
         htT = keep.tile([P, ROW_TILES, HALVES, 2, P], BF16, name="htT")
         UT = {}
@@ -194,31 +195,24 @@ def tile_treelstm_pb_kernel(
                 out=z_codes[:, j, :].bitcast(FP8X4), scales=z_scales[:, j, :], in_=z_grouped[:, j, :]
             )
 
-        def plain_product(j, x):
+        def plain_product(j, x, cols, with_bias):
             acc = new_bank()
-            bias_in_group = x == "o"
-            if bias_in_group:
+            width = cols.stop - cols.start
+            if with_bias:
                 nc.tensor.matmul(
-                    out=acc[:], lhsT=ones[:], rhs=bias_rows[:, column[x], :], start=True, stop=False
+                    out=acc[:, :width], lhsT=ones[:], rhs=bias_rows[:, column[x], cols], start=True, stop=False
                 )
             UT_pairs = UT[x][:].rearrange("q u (n e) -> q u n e", e=2)
             for u in range(HALVES):
                 for e in range(2):
                     nc.tensor.matmul(
-                        out=acc[:],
+                        out=acc[:, :width],
                         lhsT=htT[:, j, u, e, :],
-                        rhs=UT_pairs[:, u, :, e],
-                        start=(u == 0 and e == 0 and not bias_in_group),
+                        rhs=UT_pairs[:, u, cols, e],
+                        start=(u == 0 and e == 0 and not with_bias),
                         stop=(u == HALVES - 1 and e == 1),
                     )
-            if not bias_in_group:
-                nc.vector.tensor_tensor(
-                    out=partial[(j, x)][:], in0=acc[:], in1=bias_bc[:, column[x], :], op=ADD
-                )
-            elif j == 0:
-                nc.scalar.copy(out=partial[(j, x)][:], in_=acc[:])
-            else:
-                nc.vector.tensor_copy(out=partial[(j, x)][:], in_=acc[:])
+            return acc
 
         def mx_product(j, x):
             acc = new_bank()
@@ -232,43 +226,72 @@ def tile_treelstm_pb_kernel(
                     start=(g == 0),
                     stop=(g == PASSES - 1),
                 )
+            return acc
+
+        ALL = slice(0, CH)
+
+        def plain_then_bias(j, x):
+            acc = plain_product(j, x, ALL, False)
+            nc.vector.tensor_tensor(out=partial[(j, x)][:], in0=acc[:], in1=bias_bc[:, column[x], :], op=ADD)
+
+        def mx_then_gate(j, x):
+            acc = mx_product(j, x)
             nc.vector.tensor_tensor(out=partial[(j, x)][:], in0=acc[:], in1=partial[(j, x)][:], op=ADD)
             nc.scalar.activation(out=gate[(j, x)][:], in_=partial[(j, x)][:], func=func[x])
 
-        def cell_state(j, engine):
-            engine.tensor_tensor(out=iu[j][:], in0=gate[(j, "i")][:], in1=gate[(j, "u")][:], op=MULT)
-            engine.tensor_tensor(out=result[j][:, CH:], in0=iu[j][:], in1=fc_sb[:, j, :], op=ADD)
+        def store_c(j):
             nc.sync.dma_start(out=out_rows[:, j, CH:], in_=result[j][:, CH:])
 
         def tanh_cell(j):
             nc.scalar.activation(out=tanh_c[j][:], in_=result[j][:, CH:], func=TANH)
 
-        def hidden(j):
-            nc.vector.tensor_tensor(out=result[j][:, :CH], in0=gate[(j, "o")][:], in1=tanh_c[j][:], op=MULT)
-            nc.sync.dma_start(out=out_rows[:, j, :CH], in_=result[j][:, :CH])
+        def gate_o(j, cols, acc):
+            width = cols.stop - cols.start
+            nc.vector.tensor_tensor(
+                out=partial[(j, "o")][:, cols], in0=acc[:, :width], in1=partial[(j, "o")][:, cols], op=ADD
+            )
+            nc.scalar.activation(out=gate[(j, "o")][:, cols], in_=partial[(j, "o")][:, cols], func=SIGMOID)
+
+        def hidden(j, cols):
+            nc.vector.tensor_tensor(
+                out=result[j][:, cols], in0=gate[(j, "o")][:, cols], in1=tanh_c[j][:, cols], op=MULT
+            )
+            nc.sync.dma_start(out=out_rows[:, j, cols], in_=result[j][:, cols])
 
         transpose_ht()
         broadcast_bias("u")
         broadcast_bias("i")
         transpose_U("u", (nc.scalar.copy, nc.vector.tensor_copy))
+        transpose_U("i", (nc.scalar.copy, nc.vector.tensor_copy))
+        plain_then_bias(0, "u")
         transpose_z(0, nc.scalar.copy)
         quantise_z(0)
-        for x, following in (("u", "i"), ("i", "o")):
-            plain_product(0, x)
-            if x == "u":
-                transpose_z(1, nc.scalar.copy)
-                quantise_z(1)
-            transpose_U(following, (nc.scalar.copy, nc.scalar.copy))
-            plain_product(1, x)
-            mx_product(0, x)
-            mx_product(1, x)
-        cell_state(0, nc.gpsimd)
-        plain_product(0, "o")
-        cell_state(1, nc.vector)
-        tanh_cell(1)
-        plain_product(1, "o")
+        transpose_z(1, nc.scalar.copy)
+        plain_then_bias(0, "i")
+        mx_then_gate(0, "u")
+        mx_then_gate(0, "i")
+        quantise_z(1)
+        transpose_U("o", (nc.scalar.copy, nc.scalar.copy))
+        nc.vector.tensor_tensor(out=iu[0][:], in0=gate[(0, "i")][:], in1=gate[(0, "u")][:], op=MULT)
+        nc.gpsimd.tensor_tensor(out=result[0][:, CH:], in0=iu[0][:], in1=fc_sb[:, 0, :], op=ADD)
+        store_c(0)
+        plain_then_bias(1, "u")
+        plain_then_bias(1, "i")
         tanh_cell(0)
-        mx_product(0, "o")
-        mx_product(1, "o")
-        hidden(0)
-        hidden(1)
+        mx_then_gate(1, "u")
+        mx_then_gate(1, "i")
+        for j in range(ROW_TILES):
+            acc = mx_product(j, "o")
+            nc.scalar.copy(out=partial[(j, "o")][:], in_=acc[:])
+        nc.vector.tensor_tensor(out=iu[1][:], in0=gate[(1, "i")][:], in1=gate[(1, "u")][:], op=MULT)
+        nc.vector.tensor_tensor(out=result[1][:, CH:], in0=iu[1][:], in1=fc_sb[:, 1, :], op=ADD)
+        store_c(1)
+        tanh_cell(1)
+        gate_o(0, ALL, plain_product(0, "o", ALL, True))
+        LEFT = slice(0, CH // 2)
+        RIGHT = slice(CH // 2, CH)
+        gate_o(1, LEFT, plain_product(1, "o", LEFT, True))
+        gate_o(1, RIGHT, plain_product(1, "o", RIGHT, True))
+        hidden(0, ALL)
+        hidden(1, LEFT)
+        hidden(1, RIGHT)

@@ -245,13 +245,6 @@ def tile_treelstm_pb_kernel(
         def tanh_cell(j):
             nc.scalar.activation(out=tanh_c[j][:], in_=result[j][:, CH:], func=TANH)
 
-        def gate_o(j, cols, acc):
-            width = cols.stop - cols.start
-            nc.vector.tensor_tensor(
-                out=partial[(j, "o")][:, cols], in0=acc[:, :width], in1=partial[(j, "o")][:, cols], op=ADD
-            )
-            nc.scalar.activation(out=gate[(j, "o")][:, cols], in_=partial[(j, "o")][:, cols], func=SIGMOID)
-
         def hidden(j, cols):
             nc.vector.tensor_tensor(
                 out=result[j][:, cols], in0=gate[(j, "o")][:, cols], in1=tanh_c[j][:, cols], op=MULT
@@ -280,18 +273,32 @@ def tile_treelstm_pb_kernel(
         tanh_cell(0)
         mx_then_gate(1, "u")
         mx_then_gate(1, "i")
-        for j in range(ROW_TILES):
-            acc = mx_product(j, "o")
-            nc.scalar.copy(out=partial[(j, "o")][:], in_=acc[:])
+        LEFT = slice(0, CH // 2)
+        RIGHT = slice(CH // 2, CH)
+
+        def add_o(j, cols, acc):
+            width = cols.stop - cols.start
+            nc.vector.tensor_tensor(
+                out=partial[(j, "o")][:, cols], in0=acc[:, :width], in1=partial[(j, "o")][:, cols], op=ADD
+            )
+
+        def sigmoid_o(j, cols):
+            nc.scalar.activation(out=gate[(j, "o")][:, cols], in_=partial[(j, "o")][:, cols], func=SIGMOID)
+
+        acc = mx_product(0, "o")
+        nc.vector.tensor_copy(out=partial[(0, "o")][:], in_=acc[:])
+        add_o(0, ALL, plain_product(0, "o", ALL, True))
+        acc = mx_product(1, "o")
+        nc.scalar.copy(out=partial[(1, "o")][:], in_=acc[:])
+        sigmoid_o(0, ALL)
         nc.vector.tensor_tensor(out=iu[1][:], in0=gate[(1, "i")][:], in1=gate[(1, "u")][:], op=MULT)
+        add_o(1, LEFT, plain_product(1, "o", LEFT, True))
+        sigmoid_o(1, LEFT)
         nc.vector.tensor_tensor(out=result[1][:, CH:], in0=iu[1][:], in1=fc_sb[:, 1, :], op=ADD)
         store_c(1)
         tanh_cell(1)
-        gate_o(0, ALL, plain_product(0, "o", ALL, True))
-        LEFT = slice(0, CH // 2)
-        RIGHT = slice(CH // 2, CH)
-        gate_o(1, LEFT, plain_product(1, "o", LEFT, True))
-        gate_o(1, RIGHT, plain_product(1, "o", RIGHT, True))
+        add_o(1, RIGHT, plain_product(1, "o", RIGHT, True))
+        sigmoid_o(1, RIGHT)
         hidden(0, ALL)
         hidden(1, LEFT)
         hidden(1, RIGHT)

@@ -106,11 +106,11 @@ def tile_treelstm_pb_kernel(
         load_U("u")
         load_U("i")
         nc.sync.dma_start(out=z_sb[:], in_=z0.rearrange("(p j) k -> p j k", j=ROW_TILES))
+        load_U("o")
         load_scales("u")
         load_words("u")
         load_scales("i")
         load_words("i")
-        load_U("o")
         load_scales("o")
         load_words("o")
         nc.sync.dma_start(out=fc_sb[:], in_=fc_sum.rearrange("(p j) k -> p j k", j=ROW_TILES))
@@ -120,6 +120,7 @@ def tile_treelstm_pb_kernel(
         for x in GATES:
             UT[x] = keep.tile([P, HALVES, 2 * CH], BF16, name="UT_" + x)
         bias_bc = keep.tile([P, 3, CH], F32, name="bias_bc")
+        z_sorted = keep.tile([P, ROW_TILES, SIZE], BF16, name="z_sorted")
         z_grouped = keep.tile([P, ROW_TILES, PASSES * P * 4], BF16, name="z_grouped", align_bytes=64)
         z_codes = keep.tile([P, ROW_TILES, PASSES * P], U32, name="z_codes", align_bytes=64)
         z_scales = keep.tile([P, ROW_TILES, PASSES * P], U8, name="z_scales", align_bytes=64)
@@ -174,17 +175,21 @@ def tile_treelstm_pb_kernel(
                     in_=bank[:].rearrange("q (t p) -> q p t", t=4),
                 )
 
+        def sort_z(j):
+            nc.scalar.copy(
+                out=z_sorted[:].bitcast(F32)[:, j, :].rearrange("p (g u q) -> p g u q", g=PASSES, u=2),
+                in_=z_sb[:].bitcast(F32)[:, j, :].rearrange("p (g q u) -> p g u q", g=PASSES, u=2),
+            )
+
         def transpose_z(j, copy):
             bank = new_bank()
-            z_words = z_sb[:].bitcast(F32)
-            for g in range(PASSES):
-                for u in range(2):
-                    a = 2 * g + u
-                    nc.tensor.transpose(
-                        out=bank[:, a * P : (a + 1) * P],
-                        in_=z_words[:, j, 256 * g + u : 256 * (g + 1) : 2],
-                        identity=ident[:],
-                    )
+            z_words = z_sorted[:].bitcast(F32)
+            for a in range(2 * PASSES):
+                nc.tensor.transpose(
+                    out=bank[:, a * P : (a + 1) * P],
+                    in_=z_words[:, j, a * P : (a + 1) * P],
+                    identity=ident[:],
+                )
             copy(
                 out=z_grouped[:, j, :].bitcast(F32).rearrange("q (g b u) -> q g b u", g=PASSES, u=2),
                 in_=bank[:].rearrange("q (g u b) -> q g b u", g=PASSES, u=2),
@@ -239,6 +244,15 @@ def tile_treelstm_pb_kernel(
             nc.vector.tensor_tensor(out=partial[(j, x)][:], in0=acc[:], in1=partial[(j, x)][:], op=ADD)
             nc.scalar.activation(out=gate[(j, x)][:], in_=partial[(j, x)][:], func=func[x])
 
+        def mx_then_bias(j, x):
+            acc = mx_product(j, x)
+            nc.vector.tensor_tensor(out=partial[(j, x)][:], in0=acc[:], in1=bias_bc[:, column[x], :], op=ADD)
+
+        def plain_then_gate(j, x):
+            acc = plain_product(j, x, ALL, False)
+            nc.vector.tensor_tensor(out=partial[(j, x)][:], in0=acc[:], in1=partial[(j, x)][:], op=ADD)
+            nc.scalar.activation(out=gate[(j, x)][:], in_=partial[(j, x)][:], func=func[x])
+
         def store_c(j):
             nc.sync.dma_start(out=out_rows[:, j, CH:], in_=result[j][:, CH:])
 
@@ -256,23 +270,24 @@ def tile_treelstm_pb_kernel(
         broadcast_bias("i")
         transpose_U("u", (nc.scalar.copy, nc.vector.tensor_copy))
         transpose_U("i", (nc.scalar.copy, nc.vector.tensor_copy))
+        sort_z(0)
+        sort_z(1)
         plain_then_bias(0, "u")
+        plain_then_bias(0, "i")
         transpose_z(0, nc.scalar.copy)
         quantise_z(0)
         transpose_z(1, nc.scalar.copy)
-        plain_then_bias(0, "i")
-        mx_then_gate(0, "u")
-        mx_then_gate(0, "i")
         quantise_z(1)
         transpose_U("o", (nc.scalar.copy, nc.scalar.copy))
-        nc.vector.tensor_tensor(out=iu[0][:], in0=gate[(0, "i")][:], in1=gate[(0, "u")][:], op=MULT)
-        nc.gpsimd.tensor_tensor(out=result[0][:, CH:], in0=iu[0][:], in1=fc_sb[:, 0, :], op=ADD)
-        store_c(0)
         plain_then_bias(1, "u")
-        plain_then_bias(1, "i")
-        tanh_cell(0)
+        mx_then_gate(0, "u")
+        mx_then_gate(0, "i")
         mx_then_gate(1, "u")
-        mx_then_gate(1, "i")
+        mx_then_bias(1, "i")
+        nc.gpsimd.tensor_tensor(out=iu[0][:], in0=gate[(0, "i")][:], in1=gate[(0, "u")][:], op=MULT)
+        plain_then_gate(1, "i")
+        nc.vector.tensor_tensor(out=result[0][:, CH:], in0=iu[0][:], in1=fc_sb[:, 0, :], op=ADD)
+        store_c(0)
         LEFT = slice(0, CH // 2)
         RIGHT = slice(CH // 2, CH)
 
@@ -286,17 +301,18 @@ def tile_treelstm_pb_kernel(
             nc.scalar.activation(out=gate[(j, "o")][:, cols], in_=partial[(j, "o")][:, cols], func=SIGMOID)
 
         acc = mx_product(0, "o")
-        nc.vector.tensor_copy(out=partial[(0, "o")][:], in_=acc[:])
+        nc.scalar.copy(out=partial[(0, "o")][:], in_=acc[:])
+        tanh_cell(0)
+        nc.vector.tensor_tensor(out=iu[1][:], in0=gate[(1, "i")][:], in1=gate[(1, "u")][:], op=MULT)
         add_o(0, ALL, plain_product(0, "o", ALL, True))
         acc = mx_product(1, "o")
         nc.scalar.copy(out=partial[(1, "o")][:], in_=acc[:])
         sigmoid_o(0, ALL)
-        nc.vector.tensor_tensor(out=iu[1][:], in0=gate[(1, "i")][:], in1=gate[(1, "u")][:], op=MULT)
-        add_o(1, LEFT, plain_product(1, "o", LEFT, True))
-        sigmoid_o(1, LEFT)
         nc.vector.tensor_tensor(out=result[1][:, CH:], in0=iu[1][:], in1=fc_sb[:, 1, :], op=ADD)
         store_c(1)
         tanh_cell(1)
+        add_o(1, LEFT, plain_product(1, "o", LEFT, True))
+        sigmoid_o(1, LEFT)
         add_o(1, RIGHT, plain_product(1, "o", RIGHT, True))
         sigmoid_o(1, RIGHT)
         hidden(0, ALL)

@@ -96,7 +96,8 @@ def tile_treelstm_pb_kernel(
             )
 
         bias_in = keep.tile([1, 3, CH], BF16, name="bias_in")
-        nc.sync.dma_start(out=ht_sb[:], in_=h_tilde.rearrange("(p j) k -> p j k", j=ROW_TILES))
+        ht_rows = h_tilde.rearrange("(p j) k -> p j k", j=ROW_TILES)
+        nc.sync.dma_start(out=ht_sb[:, 0, :], in_=ht_rows[:, 0, :])
         for x in GATES:
             nc.sync.dma_start(
                 out=bias_in[0:1, column[x], :], in_=b_in[x].rearrange("(o n) -> o n", o=1)
@@ -106,6 +107,7 @@ def tile_treelstm_pb_kernel(
         load_U("u")
         load_U("i")
         nc.sync.dma_start(out=z_sb[:], in_=z0.rearrange("(p j) k -> p j k", j=ROW_TILES))
+        nc.sync.dma_start(out=ht_sb[:, 1, :], in_=ht_rows[:, 1, :])
         load_U("o")
         load_scales("u")
         load_words("u")
@@ -139,20 +141,18 @@ def tile_treelstm_pb_kernel(
             bank = psum.tile([P, BANK], F32, name="bank")
             return bank
 
-        def transpose_ht():
+        def transpose_ht(j, copy):
             bank = new_bank()
             ht_words = ht_sb[:].bitcast(F32)
-            for j in range(ROW_TILES):
-                for u in range(HALVES):
-                    a = j * HALVES + u
-                    nc.tensor.transpose(
-                        out=bank[:, a * P : (a + 1) * P],
-                        in_=ht_words[:, j, u * P : (u + 1) * P],
-                        identity=ident[:],
-                    )
-            nc.vector.tensor_copy(
-                out=htT[:].rearrange("q j u e p -> q (j u) e p"),
-                in_=bank[:].bitcast(BF16).rearrange("q (a p e) -> q a e p", a=ROW_TILES * HALVES, e=2),
+            for u in range(HALVES):
+                nc.tensor.transpose(
+                    out=bank[:, u * P : (u + 1) * P],
+                    in_=ht_words[:, j, u * P : (u + 1) * P],
+                    identity=ident[:],
+                )
+            copy(
+                out=htT[:, j, :, :, :],
+                in_=bank[:, : HALVES * P].bitcast(BF16).rearrange("q (u p e) -> q u e p", u=HALVES, e=2),
             )
 
         def broadcast_bias(x):
@@ -265,7 +265,7 @@ def tile_treelstm_pb_kernel(
             )
             nc.sync.dma_start(out=out_rows[:, j, cols], in_=result[j][:, cols])
 
-        transpose_ht()
+        transpose_ht(0, nc.vector.tensor_copy)
         broadcast_bias("u")
         broadcast_bias("i")
         transpose_U("u", (nc.scalar.copy, nc.vector.tensor_copy))
@@ -274,6 +274,7 @@ def tile_treelstm_pb_kernel(
         sort_z(1)
         plain_then_bias(0, "u")
         plain_then_bias(0, "i")
+        transpose_ht(1, nc.scalar.copy)
         transpose_z(0, nc.scalar.copy)
         quantise_z(0)
         transpose_z(1, nc.scalar.copy)

@@ -22,6 +22,7 @@ PASSES = SIZE // (4 * P)
 HALVES = CH // (2 * P)
 BANK = 512
 GATES = ("u", "i", "o")
+CHUNKS = 2
 
 FLOPS = 2 * 256 * (3 * CH) * (SIZE + CH)
 
@@ -76,11 +77,16 @@ def tile_treelstm_pb_kernel(
         U_sb = {}
         w_words = {}
         for x in GATES:
-            U_sb[x] = keep.tile([P, 4, CH], BF16, name="U_sb_" + x)
+            U_sb[x] = keep.tile([P, CHUNKS, 2, CH], BF16, name="U_sb_" + x)
             w_words[x] = keep.tile([P, PASSES, 4 * CH], U8, name="w_words_" + x, align_bytes=64)
 
-        def load_U(x):
-            nc.sync.dma_start(out=U_sb[x][:], in_=U_in[x].rearrange("(p t) k -> p t k", t=4))
+        def load_U(x, pieces):
+            if pieces == 1:
+                nc.sync.dma_start(out=U_sb[x][:], in_=U_in[x].rearrange("(c p t) k -> p c t k", c=CHUNKS, t=2))
+            else:
+                chunks = U_in[x].rearrange("(c p t) k -> c p t k", c=CHUNKS, t=2)
+                for c in range(CHUNKS):
+                    nc.sync.dma_start(out=U_sb[x][:, c, :, :], in_=chunks[c])
 
         def load_scales(x):
             for quadrant in range(4):
@@ -104,11 +110,11 @@ def tile_treelstm_pb_kernel(
             )
         nc.vector.tensor_copy(out=bias_rows[0:1, :, :], in_=bias_in[:])
         nc.scalar.activation(out=warm_out[:], in_=warm_in[:], func=SIGMOID)
-        load_U("u")
-        load_U("i")
+        load_U("u", 1)
+        load_U("i", CHUNKS)
         nc.sync.dma_start(out=z_sb[:], in_=z0.rearrange("(p j) k -> p j k", j=ROW_TILES))
         nc.sync.dma_start(out=ht_sb[:, 1, :], in_=ht_rows[:, 1, :])
-        load_U("o")
+        load_U("o", 1)
         load_scales("u")
         load_words("u")
         load_scales("i")
@@ -162,17 +168,21 @@ def tile_treelstm_pb_kernel(
 
         def transpose_U(x, copies):
             U_words = U_sb[x][:].bitcast(F32)
-            for u in range(HALVES):
+            UT_words = UT[x][:].bitcast(F32)
+            span = CH // CHUNKS
+            for c in range(CHUNKS):
                 bank = new_bank()
-                for t in range(4):
-                    nc.tensor.transpose(
-                        out=bank[:, t * P : (t + 1) * P],
-                        in_=U_words[:, t, u * P : (u + 1) * P],
-                        identity=ident[:],
-                    )
-                copies[u](
-                    out=UT[x][:, u, :].bitcast(F32).rearrange("q (p t) -> q p t", t=4),
-                    in_=bank[:].rearrange("q (t p) -> q p t", t=4),
+                for t in range(2):
+                    for u in range(HALVES):
+                        a = t * HALVES + u
+                        nc.tensor.transpose(
+                            out=bank[:, a * P : (a + 1) * P],
+                            in_=U_words[:, c, t, u * P : (u + 1) * P],
+                            identity=ident[:],
+                        )
+                copies[c](
+                    out=UT_words[:, :, c * span : (c + 1) * span].rearrange("q u (p t) -> q u p t", t=2),
+                    in_=bank[:].rearrange("q (t u p) -> q u p t", t=2, u=HALVES),
                 )
 
         def sort_z(j):

@@ -23,6 +23,7 @@ HALVES = CH // (2 * P)
 BANK = 512
 GATES = ("u", "i", "o")
 CHUNKS = 2
+QUARTERS = 4
 
 FLOPS = 2 * 256 * (3 * CH) * (SIZE + CH)
 
@@ -59,21 +60,22 @@ def tile_treelstm_pb_kernel(
         psum = ctx.enter_context(tc.psum_pool(name="psum", bufs=8))
         ctx.enter_context(tc.manual_schedule())
 
-        bias_rows = keep.tile([P, 3, CH], BF16, name="bias_rows")
-        nc.vector.memset(bias_rows[:].bitcast(I32), 0)
+        ones = keep.tile([P, P], F32, name="ones")
+        nc.vector.memset(ones[:], 1.0)
         warm_in = keep.tile([P, 1], F32, name="warm_in")
         warm_out = keep.tile([P, 1], F32, name="warm_out")
         nc.vector.memset(warm_in[:], 0.0)
-        ones = keep.tile([P, P], BF16, name="ones")
-        nc.vector.memset(ones[:], 1.0)
         w_planes = keep.tile([P, 3, CH], U8, name="w_planes", align_bytes=64)
         nc.vector.memset(w_planes[:].bitcast(I32), 0)
         ident = keep.tile([P, P], F32, name="ident")
         make_identity(nc, ident[:])
+        ident_half = keep.tile([P, P], BF16, name="ident_half")
+        make_identity(nc, ident_half[:])
 
         ht_sb = keep.tile([P, ROW_TILES, CH], BF16, name="ht_sb")
         z_sb = keep.tile([P, ROW_TILES, SIZE], BF16, name="z_sb")
         fc_sb = keep.tile([P, ROW_TILES, CH], BF16, name="fc_sb")
+        b_cols = keep.tile([P, 3, 16], BF16, name="b_cols")
         U_sb = {}
         w_words = {}
         for x in GATES:
@@ -88,6 +90,9 @@ def tile_treelstm_pb_kernel(
                 for c in range(CHUNKS):
                     nc.sync.dma_start(out=U_sb[x][:, c, :, :], in_=chunks[c])
 
+        def load_bias(x):
+            nc.sync.dma_start(out=b_cols[:, column[x], :QUARTERS], in_=b_in[x].rearrange("(p c) -> p c", c=QUARTERS))
+
         def load_scales(x):
             for quadrant in range(4):
                 nc.sync.dma_start(
@@ -101,24 +106,22 @@ def tile_treelstm_pb_kernel(
                 in_=words_in[x].rearrange("g p n t -> p g (n t)").bitcast(I32),
             )
 
-        bias_in = keep.tile([1, 3, CH], BF16, name="bias_in")
         ht_rows = h_tilde.rearrange("(p j) k -> p j k", j=ROW_TILES)
+        z_rows = z0.rearrange("(p j) k -> p j k", j=ROW_TILES)
         nc.sync.dma_start(out=ht_sb[:, 0, :], in_=ht_rows[:, 0, :])
-        for x in GATES:
-            nc.sync.dma_start(
-                out=bias_in[0:1, column[x], :], in_=b_in[x].rearrange("(o n) -> o n", o=1)
-            )
-        nc.vector.tensor_copy(out=bias_rows[0:1, :, :], in_=bias_in[:])
         nc.scalar.activation(out=warm_out[:], in_=warm_in[:], func=SIGMOID)
-        load_U("u", 1)
-        load_U("i", CHUNKS)
-        nc.sync.dma_start(out=z_sb[:], in_=z0.rearrange("(p j) k -> p j k", j=ROW_TILES))
+        load_U("u", CHUNKS)
         nc.sync.dma_start(out=ht_sb[:, 1, :], in_=ht_rows[:, 1, :])
-        load_U("o", 1)
+        for x in GATES:
+            load_bias(x)
+        load_U("i", CHUNKS)
+        for j in range(ROW_TILES):
+            nc.sync.dma_start(out=z_sb[:, j, :], in_=z_rows[:, j, :])
         load_scales("u")
         load_words("u")
         load_scales("i")
         load_words("i")
+        load_U("o", 1)
         load_scales("o")
         load_words("o")
         nc.sync.dma_start(out=fc_sb[:], in_=fc_sum.rearrange("(p j) k -> p j k", j=ROW_TILES))
@@ -127,7 +130,7 @@ def tile_treelstm_pb_kernel(
         UT = {}
         for x in GATES:
             UT[x] = keep.tile([P, HALVES, 2 * CH], BF16, name="UT_" + x)
-        bias_bc = keep.tile([P, 3, CH], F32, name="bias_bc")
+        bias_bc = keep.tile([P, 3, CH], BF16, name="bias_bc")
         z_sorted = keep.tile([P, ROW_TILES, SIZE], BF16, name="z_sorted")
         z_grouped = keep.tile([P, ROW_TILES, PASSES * P * 4], BF16, name="z_grouped", align_bytes=64)
         z_codes = keep.tile([P, ROW_TILES, PASSES * P], U32, name="z_codes", align_bytes=64)
@@ -147,6 +150,10 @@ def tile_treelstm_pb_kernel(
             bank = psum.tile([P, BANK], F32, name="bank")
             return bank
 
+        def warm_up(bank, count):
+            for n in range(count):
+                nc.tensor.matmul(out=bank[:, :P], lhsT=ones[:], rhs=ones[:], start=True, stop=True)
+
         def transpose_ht(j, copy):
             bank = new_bank()
             ht_words = ht_sb[:].bitcast(F32)
@@ -161,34 +168,46 @@ def tile_treelstm_pb_kernel(
                 in_=bank[:, : HALVES * P].bitcast(BF16).rearrange("q (u p e) -> q u e p", u=HALVES, e=2),
             )
 
-        def broadcast_bias(x):
+        def broadcast_bias(x, copy):
             bank = new_bank()
-            nc.tensor.matmul(out=bank[:], lhsT=ones[:], rhs=bias_rows[:, column[x], :], start=True, stop=True)
-            nc.scalar.copy(out=bias_bc[:, column[x], :], in_=bank[:])
+            rows = bank[:].bitcast(BF16)
+            for c in range(QUARTERS):
+                nc.tensor.transpose(
+                    out=rows[:, c * P : (c + 1) * P],
+                    in_=b_cols[:, column[x], c : c + 1].to_broadcast([P, P]),
+                    identity=ident_half[:],
+                )
+            copy(
+                out=bias_bc[:, column[x], :].rearrange("q (p c) -> q p c", c=QUARTERS),
+                in_=rows[:, :CH].rearrange("q (c p) -> q p c", c=QUARTERS),
+            )
 
-        def transpose_U(x, copies):
+        def transpose_U(x, c, copy):
             U_words = U_sb[x][:].bitcast(F32)
             UT_words = UT[x][:].bitcast(F32)
             span = CH // CHUNKS
-            for c in range(CHUNKS):
-                bank = new_bank()
-                for t in range(2):
-                    for u in range(HALVES):
-                        a = t * HALVES + u
-                        nc.tensor.transpose(
-                            out=bank[:, a * P : (a + 1) * P],
-                            in_=U_words[:, c, t, u * P : (u + 1) * P],
-                            identity=ident[:],
-                        )
-                copies[c](
-                    out=UT_words[:, :, c * span : (c + 1) * span].rearrange("q u (p t) -> q u p t", t=2),
-                    in_=bank[:].rearrange("q (t u p) -> q u p t", t=2, u=HALVES),
-                )
+            bank = new_bank()
+            for t in range(2):
+                for u in range(HALVES):
+                    a = t * HALVES + u
+                    nc.tensor.transpose(
+                        out=bank[:, a * P : (a + 1) * P],
+                        in_=U_words[:, c, t, u * P : (u + 1) * P],
+                        identity=ident[:],
+                    )
+            copy(
+                out=UT_words[:, :, c * span : (c + 1) * span].rearrange("q u (p t) -> q u p t", t=2),
+                in_=bank[:].rearrange("q (t u p) -> q u p t", t=2, u=HALVES),
+            )
 
         def sort_z(j):
-            nc.scalar.copy(
-                out=z_sorted[:].bitcast(F32)[:, j, :].rearrange("p (g u q) -> p g u q", g=PASSES, u=2),
-                in_=z_sb[:].bitcast(F32)[:, j, :].rearrange("p (g q u) -> p g u q", g=PASSES, u=2),
+            nc.gpsimd.tensor_scalar(
+                out=z_sorted[:, j, :].rearrange("p (u q e) -> p u q e", u=2, e=2),
+                in0=z_sb[:, j, :].rearrange("p (q u e) -> p u q e", u=2, e=2),
+                scalar1=1.0,
+                scalar2=0.0,
+                op0=MULT,
+                op1=ADD,
             )
 
         def transpose_z(j, copy):
@@ -202,7 +221,7 @@ def tile_treelstm_pb_kernel(
                 )
             copy(
                 out=z_grouped[:, j, :].bitcast(F32).rearrange("q (g b u) -> q g b u", g=PASSES, u=2),
-                in_=bank[:].rearrange("q (g u b) -> q g b u", g=PASSES, u=2),
+                in_=bank[:].rearrange("q (u g b) -> q g b u", g=PASSES, u=2),
             )
 
         def quantise_z(j):
@@ -210,24 +229,17 @@ def tile_treelstm_pb_kernel(
                 out=z_codes[:, j, :].bitcast(FP8X4), scales=z_scales[:, j, :], in_=z_grouped[:, j, :]
             )
 
-        def plain_product(j, x, cols, with_bias):
-            acc = new_bank()
-            width = cols.stop - cols.start
-            if with_bias:
-                nc.tensor.matmul(
-                    out=acc[:, :width], lhsT=ones[:], rhs=bias_rows[:, column[x], cols], start=True, stop=False
-                )
+        def plain_product(j, x, acc, cols):
             UT_pairs = UT[x][:].rearrange("q u (n e) -> q u n e", e=2)
             for u in range(HALVES):
                 for e in range(2):
                     nc.tensor.matmul(
-                        out=acc[:, :width],
+                        out=acc[:, cols],
                         lhsT=htT[:, j, u, e, :],
                         rhs=UT_pairs[:, u, cols, e],
-                        start=(u == 0 and e == 0 and not with_bias),
+                        start=(u == 0 and e == 0),
                         stop=(u == HALVES - 1 and e == 1),
                     )
-            return acc
 
         def mx_product(j, x):
             acc = new_bank()
@@ -244,26 +256,25 @@ def tile_treelstm_pb_kernel(
             return acc
 
         ALL = slice(0, CH)
+        LEFT = slice(0, CH // 2)
+        RIGHT = slice(CH // 2, CH)
 
-        def plain_then_bias(j, x):
-            acc = plain_product(j, x, ALL, False)
+        def add_bias(j, x, acc):
             nc.vector.tensor_tensor(out=partial[(j, x)][:], in0=acc[:], in1=bias_bc[:, column[x], :], op=ADD)
 
-        def mx_then_gate(j, x):
-            acc = mx_product(j, x)
-            nc.vector.tensor_tensor(out=partial[(j, x)][:], in0=acc[:], in1=partial[(j, x)][:], op=ADD)
-            nc.scalar.activation(out=gate[(j, x)][:], in_=partial[(j, x)][:], func=func[x])
+        def add_partial(j, x, acc, cols):
+            nc.vector.tensor_tensor(
+                out=partial[(j, x)][:, cols], in0=acc[:, cols], in1=partial[(j, x)][:, cols], op=ADD
+            )
 
-        def mx_then_bias(j, x):
-            acc = mx_product(j, x)
-            nc.vector.tensor_tensor(out=partial[(j, x)][:], in0=acc[:], in1=bias_bc[:, column[x], :], op=ADD)
+        def apply(j, x, cols):
+            nc.scalar.activation(out=gate[(j, x)][:, cols], in_=partial[(j, x)][:, cols], func=func[x])
 
-        def plain_then_gate(j, x):
-            acc = plain_product(j, x, ALL, False)
-            nc.vector.tensor_tensor(out=partial[(j, x)][:], in0=acc[:], in1=partial[(j, x)][:], op=ADD)
-            nc.scalar.activation(out=gate[(j, x)][:], in_=partial[(j, x)][:], func=func[x])
+        def input_times_update(j, engine):
+            engine.tensor_tensor(out=iu[j][:], in0=gate[(j, "i")][:], in1=gate[(j, "u")][:], op=MULT)
 
-        def store_c(j):
+        def cell(j, engine):
+            engine.tensor_tensor(out=result[j][:, CH:], in0=iu[j][:], in1=fc_sb[:, j, :], op=ADD)
             nc.sync.dma_start(out=out_rows[:, j, CH:], in_=result[j][:, CH:])
 
         def tanh_cell(j):
@@ -275,57 +286,61 @@ def tile_treelstm_pb_kernel(
             )
             nc.sync.dma_start(out=out_rows[:, j, cols], in_=result[j][:, cols])
 
+        spare = new_bank()
+        warm_up(spare, 3)
         transpose_ht(0, nc.vector.tensor_copy)
-        broadcast_bias("u")
-        broadcast_bias("i")
-        transpose_U("u", (nc.scalar.copy, nc.vector.tensor_copy))
-        transpose_U("i", (nc.scalar.copy, nc.vector.tensor_copy))
+        warm_up(spare, 1)
+        transpose_U("u", 0, nc.scalar.copy)
+        transpose_U("u", 1, nc.vector.tensor_copy)
+        transpose_ht(1, nc.scalar.copy)
+        broadcast_bias("u", nc.scalar.copy)
+        acc = new_bank()
+        plain_product(0, "u", acc, LEFT)
+        plain_product(0, "u", acc, RIGHT)
+        add_bias(0, "u", acc)
+        transpose_U("i", 0, nc.scalar.copy)
+        transpose_U("i", 1, nc.vector.tensor_copy)
+        broadcast_bias("i", nc.scalar.copy)
         sort_z(0)
         sort_z(1)
-        plain_then_bias(0, "u")
-        plain_then_bias(0, "i")
-        transpose_ht(1, nc.scalar.copy)
+        acc = new_bank()
+        plain_product(1, "u", acc, ALL)
+        add_bias(1, "u", acc)
         transpose_z(0, nc.scalar.copy)
         quantise_z(0)
+        acc = new_bank()
+        plain_product(0, "i", acc, ALL)
+        add_bias(0, "i", acc)
         transpose_z(1, nc.scalar.copy)
         quantise_z(1)
-        transpose_U("o", (nc.scalar.copy, nc.scalar.copy))
-        plain_then_bias(1, "u")
-        mx_then_gate(0, "u")
-        mx_then_gate(0, "i")
-        mx_then_gate(1, "u")
-        mx_then_bias(1, "i")
-        nc.gpsimd.tensor_tensor(out=iu[0][:], in0=gate[(0, "i")][:], in1=gate[(0, "u")][:], op=MULT)
-        plain_then_gate(1, "i")
-        nc.vector.tensor_tensor(out=result[0][:, CH:], in0=iu[0][:], in1=fc_sb[:, 0, :], op=ADD)
-        store_c(0)
-        LEFT = slice(0, CH // 2)
-        RIGHT = slice(CH // 2, CH)
-
-        def add_o(j, cols, acc):
-            width = cols.stop - cols.start
-            nc.vector.tensor_tensor(
-                out=partial[(j, "o")][:, cols], in0=acc[:, :width], in1=partial[(j, "o")][:, cols], op=ADD
-            )
-
-        def sigmoid_o(j, cols):
-            nc.scalar.activation(out=gate[(j, "o")][:, cols], in_=partial[(j, "o")][:, cols], func=SIGMOID)
-
-        acc = mx_product(0, "o")
-        nc.scalar.copy(out=partial[(0, "o")][:], in_=acc[:])
+        broadcast_bias("o", nc.scalar.copy)
+        for j, x in ((0, "u"), (0, "i"), (1, "u")):
+            add_partial(j, x, mx_product(j, x), ALL)
+            apply(j, x, ALL)
+        input_times_update(0, nc.gpsimd)
+        cell(0, nc.gpsimd)
+        add_bias(1, "i", mx_product(1, "i"))
+        acc = new_bank()
+        plain_product(1, "i", acc, ALL)
+        add_partial(1, "i", acc, ALL)
+        transpose_U("o", 0, nc.scalar.copy)
+        apply(1, "i", ALL)
+        input_times_update(1, nc.gpsimd)
+        transpose_U("o", 1, nc.vector.tensor_copy)
         tanh_cell(0)
-        nc.vector.tensor_tensor(out=iu[1][:], in0=gate[(1, "i")][:], in1=gate[(1, "u")][:], op=MULT)
-        add_o(0, ALL, plain_product(0, "o", ALL, True))
-        acc = mx_product(1, "o")
-        nc.scalar.copy(out=partial[(1, "o")][:], in_=acc[:])
-        sigmoid_o(0, ALL)
-        nc.vector.tensor_tensor(out=result[1][:, CH:], in0=iu[1][:], in1=fc_sb[:, 1, :], op=ADD)
-        store_c(1)
+        for j in range(ROW_TILES):
+            add_bias(j, "o", mx_product(j, "o"))
+        acc = new_bank()
+        plain_product(0, "o", acc, ALL)
+        add_partial(0, "o", acc, ALL)
+        apply(0, "o", ALL)
+        cell(1, nc.vector)
         tanh_cell(1)
-        add_o(1, LEFT, plain_product(1, "o", LEFT, True))
-        sigmoid_o(1, LEFT)
-        add_o(1, RIGHT, plain_product(1, "o", RIGHT, True))
-        sigmoid_o(1, RIGHT)
+        for cols in (LEFT, RIGHT):
+            acc = new_bank()
+            plain_product(1, "o", acc, cols)
+            add_partial(1, "o", acc, cols)
+            apply(1, "o", cols)
         hidden(0, ALL)
         hidden(1, LEFT)
         hidden(1, RIGHT)

@@ -201,13 +201,9 @@ def tile_treelstm_pb_kernel(
             )
 
         def sort_z(j):
-            nc.gpsimd.tensor_scalar(
-                out=z_sorted[:, j, :].rearrange("p (u q e) -> p u q e", u=2, e=2),
-                in0=z_sb[:, j, :].rearrange("p (q u e) -> p u q e", u=2, e=2),
-                scalar1=1.0,
-                scalar2=0.0,
-                op0=MULT,
-                op1=ADD,
+            nc.vector.tensor_copy(
+                out=z_sorted[:].bitcast(F32)[:, j, :].rearrange("p (u q) -> p u q", u=2),
+                in_=z_sb[:].bitcast(F32)[:, j, :].rearrange("p (q u) -> p u q", u=2),
             )
 
         def transpose_z(j, copy):
@@ -289,7 +285,6 @@ def tile_treelstm_pb_kernel(
         spare = new_bank()
         warm_up(spare, 3)
         transpose_ht(0, nc.vector.tensor_copy)
-        warm_up(spare, 1)
         transpose_U("u", 0, nc.scalar.copy)
         transpose_U("u", 1, nc.vector.tensor_copy)
         transpose_ht(1, nc.scalar.copy)
@@ -297,12 +292,12 @@ def tile_treelstm_pb_kernel(
         acc = new_bank()
         plain_product(0, "u", acc, LEFT)
         plain_product(0, "u", acc, RIGHT)
+        sort_z(0)
+        sort_z(1)
         add_bias(0, "u", acc)
         transpose_U("i", 0, nc.scalar.copy)
         transpose_U("i", 1, nc.vector.tensor_copy)
         broadcast_bias("i", nc.scalar.copy)
-        sort_z(0)
-        sort_z(1)
         acc = new_bank()
         plain_product(1, "u", acc, ALL)
         add_bias(1, "u", acc)

@@ -23,7 +23,6 @@ HALVES = CH // (2 * P)
 BANK = 512
 GATES = ("u", "i", "o")
 CHUNKS = 2
-QUARTERS = 4
 
 FLOPS = 2 * 256 * (3 * CH) * (SIZE + CH)
 
@@ -62,6 +61,10 @@ def tile_treelstm_pb_kernel(
 
         ones = keep.tile([P, P], F32, name="ones")
         nc.vector.memset(ones[:], 1.0)
+        ones_half = keep.tile([P, P], BF16, name="ones_half")
+        nc.vector.memset(ones_half[:], 1.0)
+        bias_rows = keep.tile([P, 3, CH], BF16, name="bias_rows")
+        nc.vector.memset(bias_rows[:].bitcast(I32), 0)
         warm_in = keep.tile([P, 1], F32, name="warm_in")
         warm_out = keep.tile([P, 1], F32, name="warm_out")
         nc.vector.memset(warm_in[:], 0.0)
@@ -69,13 +72,10 @@ def tile_treelstm_pb_kernel(
         nc.vector.memset(w_planes[:].bitcast(I32), 0)
         ident = keep.tile([P, P], F32, name="ident")
         make_identity(nc, ident[:])
-        ident_half = keep.tile([P, P], BF16, name="ident_half")
-        make_identity(nc, ident_half[:])
 
         ht_sb = keep.tile([P, ROW_TILES, CH], BF16, name="ht_sb")
         z_sb = keep.tile([P, ROW_TILES, SIZE], BF16, name="z_sb")
         fc_sb = keep.tile([P, ROW_TILES, CH], BF16, name="fc_sb")
-        b_cols = keep.tile([P, 3, 16], BF16, name="b_cols")
         U_sb = {}
         w_words = {}
         for x in GATES:
@@ -91,7 +91,7 @@ def tile_treelstm_pb_kernel(
                     nc.sync.dma_start(out=U_sb[x][:, c, :, :], in_=chunks[c])
 
         def load_bias(x):
-            nc.sync.dma_start(out=b_cols[:, column[x], :QUARTERS], in_=b_in[x].rearrange("(p c) -> p c", c=QUARTERS))
+            nc.sync.dma_start(out=bias_rows[0:1, column[x], :], in_=b_in[x].rearrange("(o n) -> o n", o=1))
 
         def load_scales(x):
             for quadrant in range(4):
@@ -170,17 +170,8 @@ def tile_treelstm_pb_kernel(
 
         def broadcast_bias(x, copy):
             bank = new_bank()
-            rows = bank[:].bitcast(BF16)
-            for c in range(QUARTERS):
-                nc.tensor.transpose(
-                    out=rows[:, c * P : (c + 1) * P],
-                    in_=b_cols[:, column[x], c : c + 1].to_broadcast([P, P]),
-                    identity=ident_half[:],
-                )
-            copy(
-                out=bias_bc[:, column[x], :].rearrange("q (p c) -> q p c", c=QUARTERS),
-                in_=rows[:, :CH].rearrange("q (c p) -> q p c", c=QUARTERS),
-            )
+            nc.tensor.matmul(out=bank[:], lhsT=ones_half[:], rhs=bias_rows[:, column[x], :], start=True, stop=True)
+            copy(out=bias_bc[:, column[x], :], in_=bank[:])
 
         def transpose_U(x, c, copy):
             U_words = U_sb[x][:].bitcast(F32)

@@ -173,6 +173,23 @@ def tile_treelstm_pb_kernel(
             nc.tensor.matmul(out=bank[:], lhsT=ones_half[:], rhs=bias_rows[:, column[x], :], start=True, stop=True)
             copy(out=bias_bc[:, column[x], :], in_=bank[:])
 
+        def transpose_U_halves(x, c, copies):
+            U_words = U_sb[x][:].bitcast(F32)
+            UT_words = UT[x][:].bitcast(F32)
+            span = CH // CHUNKS
+            for u in range(HALVES):
+                bank = new_bank()
+                for t in range(2):
+                    nc.tensor.transpose(
+                        out=bank[:, t * P : (t + 1) * P],
+                        in_=U_words[:, c, t, u * P : (u + 1) * P],
+                        identity=ident[:],
+                    )
+                copies[u](
+                    out=UT_words[:, u, c * span : (c + 1) * span].rearrange("q (p t) -> q p t", t=2),
+                    in_=bank[:, : 2 * P].rearrange("q (t p) -> q p t", t=2),
+                )
+
         def transpose_U(x, c, copy):
             U_words = U_sb[x][:].bitcast(F32)
             UT_words = UT[x][:].bitcast(F32)
@@ -276,19 +293,19 @@ def tile_treelstm_pb_kernel(
         spare = new_bank()
         warm_up(spare, 3)
         transpose_ht(0, nc.vector.tensor_copy)
-        transpose_U("u", 0, nc.scalar.copy)
-        transpose_U("u", 1, nc.vector.tensor_copy)
-        transpose_ht(1, nc.scalar.copy)
+        transpose_U_halves("u", 0, (nc.scalar.copy, nc.vector.tensor_copy))
+        transpose_U_halves("u", 1, (nc.scalar.copy, nc.vector.tensor_copy))
         broadcast_bias("u", nc.scalar.copy)
+        transpose_ht(1, nc.scalar.copy)
+        broadcast_bias("i", nc.scalar.copy)
         acc = new_bank()
         plain_product(0, "u", acc, LEFT)
         plain_product(0, "u", acc, RIGHT)
         sort_z(0)
-        sort_z(1)
         add_bias(0, "u", acc)
         transpose_U("i", 0, nc.scalar.copy)
         transpose_U("i", 1, nc.vector.tensor_copy)
-        broadcast_bias("i", nc.scalar.copy)
+        sort_z(1)
         acc = new_bank()
         plain_product(1, "u", acc, ALL)
         add_bias(1, "u", acc)
@@ -311,22 +328,25 @@ def tile_treelstm_pb_kernel(
         add_partial(1, "i", acc, ALL)
         transpose_U("o", 0, nc.scalar.copy)
         apply(1, "i", ALL)
-        input_times_update(1, nc.gpsimd)
         transpose_U("o", 1, nc.vector.tensor_copy)
         tanh_cell(0)
         for j in range(ROW_TILES):
             add_bias(j, "o", mx_product(j, "o"))
+        input_times_update(1, nc.vector)
         acc = new_bank()
         plain_product(0, "o", acc, ALL)
         add_partial(0, "o", acc, ALL)
         apply(0, "o", ALL)
         cell(1, nc.vector)
         tanh_cell(1)
-        for cols in (LEFT, RIGHT):
-            acc = new_bank()
-            plain_product(1, "o", acc, cols)
-            add_partial(1, "o", acc, cols)
-            apply(1, "o", cols)
+        acc = new_bank()
+        plain_product(1, "o", acc, LEFT)
+        add_partial(1, "o", acc, LEFT)
+        apply(1, "o", LEFT)
+        acc = new_bank()
+        plain_product(1, "o", acc, RIGHT)
+        add_partial(1, "o", acc, RIGHT)
+        apply(1, "o", RIGHT)
         hidden(0, ALL)
         hidden(1, LEFT)
         hidden(1, RIGHT)

@@ -61,6 +61,8 @@ def tile_treelstm_pb_kernel(
 
         ones = keep.tile([P, P], F32, name="ones")
         nc.vector.memset(ones[:], 1.0)
+        w_planes = keep.tile([P, 3, CH], U8, name="w_planes", align_bytes=64)
+        nc.vector.memset(w_planes[:].bitcast(I32), 0)
         ones_half = keep.tile([P, P], BF16, name="ones_half")
         nc.vector.memset(ones_half[:], 1.0)
         bias_rows = keep.tile([P, 3, CH], BF16, name="bias_rows")
@@ -68,8 +70,6 @@ def tile_treelstm_pb_kernel(
         warm_in = keep.tile([P, 1], F32, name="warm_in")
         warm_out = keep.tile([P, 1], F32, name="warm_out")
         nc.vector.memset(warm_in[:], 0.0)
-        w_planes = keep.tile([P, 3, CH], U8, name="w_planes", align_bytes=64)
-        nc.vector.memset(w_planes[:].bitcast(I32), 0)
         ident = keep.tile([P, P], F32, name="ident")
         make_identity(nc, ident[:])
 
@@ -82,23 +82,19 @@ def tile_treelstm_pb_kernel(
             U_sb[x] = keep.tile([P, CHUNKS, 2, CH], BF16, name="U_sb_" + x)
             w_words[x] = keep.tile([P, PASSES, 4 * CH], U8, name="w_words_" + x, align_bytes=64)
 
-        def load_U(x, pieces):
-            if pieces == 1:
-                nc.sync.dma_start(out=U_sb[x][:], in_=U_in[x].rearrange("(c p t) k -> p c t k", c=CHUNKS, t=2))
-            else:
-                chunks = U_in[x].rearrange("(c p t) k -> c p t k", c=CHUNKS, t=2)
-                for c in range(CHUNKS):
-                    nc.sync.dma_start(out=U_sb[x][:, c, :, :], in_=chunks[c])
+        U_chunks = {x: U_in[x].rearrange("(c p t) k -> c p t k", c=CHUNKS, t=2) for x in GATES}
 
-        def load_bias(x):
-            nc.sync.dma_start(out=bias_rows[0:1, column[x], :], in_=b_in[x].rearrange("(o n) -> o n", o=1))
+        def load_U(x, c):
+            nc.sync.dma_start(out=U_sb[x][:, c, :, :], in_=U_chunks[x][c])
 
-        def load_scales(x):
-            for quadrant in range(4):
-                nc.sync.dma_start(
-                    out=w_planes[32 * quadrant : 32 * quadrant + 4 * PASSES, column[x], :].bitcast(I32),
-                    in_=scales_in[x][:, 4 * quadrant : 4 * quadrant + 4, :].bitcast(I32),
-                )
+        def load_bias(x, queue):
+            queue.dma_start(out=bias_rows[0:1, column[x], :], in_=b_in[x].rearrange("(o n) -> o n", o=1))
+
+        def load_scales(x, quadrant):
+            nc.sync.dma_start(
+                out=w_planes[32 * quadrant : 32 * quadrant + 4 * PASSES, column[x], :].bitcast(I32),
+                in_=scales_in[x][:, 4 * quadrant : 4 * quadrant + 4, :].bitcast(I32),
+            )
 
         def load_words(x):
             nc.sync.dma_start(
@@ -106,24 +102,39 @@ def tile_treelstm_pb_kernel(
                 in_=words_in[x].rearrange("g p n t -> p g (n t)").bitcast(I32),
             )
 
+        def load_z(j):
+            nc.sync.dma_start(out=z_sb[:, j, :], in_=z_rows[:, j, :])
+
         ht_rows = h_tilde.rearrange("(p j) k -> p j k", j=ROW_TILES)
         z_rows = z0.rearrange("(p j) k -> p j k", j=ROW_TILES)
         nc.sync.dma_start(out=ht_sb[:, 0, :], in_=ht_rows[:, 0, :])
         nc.scalar.activation(out=warm_out[:], in_=warm_in[:], func=SIGMOID)
-        load_U("u", CHUNKS)
+        load_bias("o", nc.gpsimd)
+        load_U("u", 0)
+        load_U("u", 1)
+        load_bias("u", nc.sync)
+        load_bias("i", nc.sync)
         nc.sync.dma_start(out=ht_sb[:, 1, :], in_=ht_rows[:, 1, :])
-        for x in GATES:
-            load_bias(x)
-        load_U("i", CHUNKS)
-        for j in range(ROW_TILES):
-            nc.sync.dma_start(out=z_sb[:, j, :], in_=z_rows[:, j, :])
-        load_scales("u")
+        load_U("i", 0)
+        load_scales("u", 0)
+        load_U("i", 1)
+        load_scales("u", 1)
+        load_z(0)
+        load_scales("u", 2)
+        load_z(1)
+        load_scales("u", 3)
         load_words("u")
-        load_scales("i")
+        load_scales("i", 0)
+        load_scales("i", 1)
         load_words("i")
-        load_U("o", 1)
-        load_scales("o")
+        load_scales("i", 2)
+        load_scales("i", 3)
+        nc.sync.dma_start(out=U_sb["o"][:], in_=U_in["o"].rearrange("(c p t) k -> p c t k", c=CHUNKS, t=2))
+        load_scales("o", 0)
+        load_scales("o", 1)
         load_words("o")
+        load_scales("o", 2)
+        load_scales("o", 3)
         nc.sync.dma_start(out=fc_sb[:], in_=fc_sum.rearrange("(p j) k -> p j k", j=ROW_TILES))
 
         htT = keep.tile([P, ROW_TILES, HALVES, 2, P], BF16, name="htT")

@@ -61,12 +61,14 @@ def tile_treelstm_pb_kernel(
 
         ones = keep.tile([P, P], F32, name="ones")
         nc.vector.memset(ones[:], 1.0)
+        bias_rows = {x: keep.tile([P, CH], BF16, name="bias_rows_" + x) for x in GATES}
+        nc.vector.memset(bias_rows["u"][:].bitcast(I32), 0)
         w_planes = keep.tile([P, 3, CH], U8, name="w_planes", align_bytes=64)
         nc.vector.memset(w_planes[:].bitcast(I32), 0)
         ones_half = keep.tile([P, P], BF16, name="ones_half")
         nc.vector.memset(ones_half[:], 1.0)
-        bias_rows = keep.tile([P, 3, CH], BF16, name="bias_rows")
-        nc.vector.memset(bias_rows[:].bitcast(I32), 0)
+        for x in ("i", "o"):
+            nc.vector.memset(bias_rows[x][:].bitcast(I32), 0)
         warm_in = keep.tile([P, 1], F32, name="warm_in")
         warm_out = keep.tile([P, 1], F32, name="warm_out")
         nc.vector.memset(warm_in[:], 0.0)
@@ -88,7 +90,7 @@ def tile_treelstm_pb_kernel(
             nc.sync.dma_start(out=U_sb[x][:, c, :, :], in_=U_chunks[x][c])
 
         def load_bias(x, queue):
-            queue.dma_start(out=bias_rows[0:1, column[x], :], in_=b_in[x].rearrange("(o n) -> o n", o=1))
+            queue.dma_start(out=bias_rows[x][0:1, :], in_=b_in[x].rearrange("(o n) -> o n", o=1))
 
         def load_scales(x, quadrant):
             nc.sync.dma_start(
@@ -111,10 +113,10 @@ def tile_treelstm_pb_kernel(
         nc.scalar.activation(out=warm_out[:], in_=warm_in[:], func=SIGMOID)
         load_bias("o", nc.gpsimd)
         load_U("u", 0)
-        load_U("u", 1)
         load_bias("u", nc.sync)
-        load_bias("i", nc.sync)
+        load_U("u", 1)
         nc.sync.dma_start(out=ht_sb[:, 1, :], in_=ht_rows[:, 1, :])
+        load_bias("i", nc.sync)
         load_U("i", 0)
         load_scales("u", 0)
         load_U("i", 1)
@@ -179,10 +181,13 @@ def tile_treelstm_pb_kernel(
                 in_=bank[:, : HALVES * P].bitcast(BF16).rearrange("q (u p e) -> q u e p", u=HALVES, e=2),
             )
 
-        def broadcast_bias(x, copy):
+        def broadcast_bias(x):
             bank = new_bank()
-            nc.tensor.matmul(out=bank[:], lhsT=ones_half[:], rhs=bias_rows[:, column[x], :], start=True, stop=True)
-            copy(out=bias_bc[:, column[x], :], in_=bank[:])
+            nc.tensor.matmul(out=bank[:], lhsT=ones_half[:], rhs=bias_rows[x][:], start=True, stop=True)
+            return bank
+
+        def keep_bias(x, bank):
+            nc.scalar.copy(out=bias_bc[:, column[x], :], in_=bank[:])
 
         def transpose_U_halves(x, c, copies):
             U_words = U_sb[x][:].bitcast(F32)
@@ -305,10 +310,11 @@ def tile_treelstm_pb_kernel(
         warm_up(spare, 3)
         transpose_ht(0, nc.vector.tensor_copy)
         transpose_U_halves("u", 0, (nc.scalar.copy, nc.vector.tensor_copy))
+        bias_u = broadcast_bias("u")
         transpose_U_halves("u", 1, (nc.scalar.copy, nc.vector.tensor_copy))
-        broadcast_bias("u", nc.scalar.copy)
+        keep_bias("u", bias_u)
         transpose_ht(1, nc.scalar.copy)
-        broadcast_bias("i", nc.scalar.copy)
+        keep_bias("i", broadcast_bias("i"))
         acc = new_bank()
         plain_product(0, "u", acc, LEFT)
         plain_product(0, "u", acc, RIGHT)
@@ -327,7 +333,7 @@ def tile_treelstm_pb_kernel(
         add_bias(0, "i", acc)
         transpose_z(1, nc.scalar.copy)
         quantise_z(1)
-        broadcast_bias("o", nc.scalar.copy)
+        keep_bias("o", broadcast_bias("o"))
         for j, x in ((0, "u"), (0, "i"), (1, "u")):
             add_partial(j, x, mx_product(j, x), ALL)
             apply(j, x, ALL)

@@ -23,6 +23,7 @@ HALVES = CH // (2 * P)
 BANK = 512
 GATES = ("u", "i", "o")
 CHUNKS = 2
+WARM_ROUNDS = 3
 
 FLOPS = 2 * 256 * (3 * CH) * (SIZE + CH)
 
@@ -163,9 +164,15 @@ def tile_treelstm_pb_kernel(
             bank = psum.tile([P, BANK], F32, name="bank")
             return bank
 
-        def warm_up(bank, count):
-            for n in range(count):
-                nc.tensor.matmul(out=bank[:, :P], lhsT=ones[:], rhs=ones[:], start=True, stop=True)
+        def warm_up():
+            bank = new_bank()
+            nc.tensor.matmul(
+                out=bank[:, : WARM_ROUNDS * P].rearrange("p (r n) -> p r n", r=WARM_ROUNDS),
+                lhsT=ones[:],
+                rhs=ones[:].unsqueeze(1).to_broadcast([P, WARM_ROUNDS, P]),
+                start=True,
+                stop=True,
+            )
 
         def transpose_ht(j, copy):
             bank = new_bank()
@@ -306,8 +313,7 @@ def tile_treelstm_pb_kernel(
             )
             nc.sync.dma_start(out=out_rows[:, j, cols], in_=result[j][:, cols])
 
-        spare = new_bank()
-        warm_up(spare, 3)
+        warm_up()
         transpose_ht(0, nc.vector.tensor_copy)
         transpose_U_halves("u", 0, (nc.scalar.copy, nc.vector.tensor_copy))
         bias_u = broadcast_bias("u")

from contextlib import ExitStack

import concourse.mybir as mybir
from concourse.masks import make_identity

F32 = mybir.dt.float32
BF16 = mybir.dt.bfloat16
I32 = mybir.dt.int32
U32 = mybir.dt.uint32
U8 = mybir.dt.uint8
FP8X4 = mybir.dt.float8_e4m3fn_x4
ADD = mybir.AluOpType.add
MULT = mybir.AluOpType.mult
SIGMOID = mybir.ActivationFunctionType.Sigmoid
TANH = mybir.ActivationFunctionType.Tanh

P = 128
ROW_TILES = 2
SIZE = 1024
CH = 512
PASSES = SIZE // (4 * P)
HALVES = CH // (2 * P)
BANK = 512
GATES = ("u", "i", "o")
CHUNKS = 2
WARM_ROUNDS = 3

FLOPS = 2 * 256 * (3 * CH) * (SIZE + CH)


def tile_treelstm_pb_kernel(
    tc,
    z0,
    h_tilde,
    fc_sum,
    W_i_words,
    W_i_scales,
    U_i,
    b_i,
    W_o_words,
    W_o_scales,
    U_o,
    b_o,
    W_u_words,
    W_u_scales,
    U_u,
    b_u,
    out,
):
    nc = tc.nc
    words_in = {"u": W_u_words, "i": W_i_words, "o": W_o_words}
    scales_in = {"u": W_u_scales, "i": W_i_scales, "o": W_o_scales}
    U_in = {"u": U_u, "i": U_i, "o": U_o}
    b_in = {"u": b_u, "i": b_i, "o": b_o}
    func = {"u": TANH, "i": SIGMOID, "o": SIGMOID}
    column = {"u": 0, "i": 1, "o": 2}

    with ExitStack() as ctx:
        keep = ctx.enter_context(tc.tile_pool(name="keep", bufs=1))
        psum = ctx.enter_context(tc.psum_pool(name="psum", bufs=8))
        ctx.enter_context(tc.manual_schedule())

        ones = keep.tile([P, P], F32, name="ones")
        nc.vector.memset(ones[:], 1.0)
        bias_rows = {x: keep.tile([P, CH], BF16, name="bias_rows_" + x) for x in GATES}
        nc.vector.memset(bias_rows["u"][:].bitcast(I32), 0)
        w_planes = keep.tile([P, 3, CH], U8, name="w_planes", align_bytes=64)
        nc.vector.memset(w_planes[:].bitcast(I32), 0)
        ones_half = keep.tile([P, P], BF16, name="ones_half")
        nc.vector.memset(ones_half[:], 1.0)
        for x in ("i", "o"):
            nc.vector.memset(bias_rows[x][:].bitcast(I32), 0)
        warm_in = keep.tile([P, 1], F32, name="warm_in")
        warm_out = keep.tile([P, 1], F32, name="warm_out")
        nc.vector.memset(warm_in[:], 0.0)
        ident = keep.tile([P, P], F32, name="ident")
        make_identity(nc, ident[:])

        ht_sb = keep.tile([P, ROW_TILES, CH], BF16, name="ht_sb")
        z_sb = keep.tile([P, ROW_TILES, SIZE], BF16, name="z_sb")
        fc_sb = keep.tile([P, ROW_TILES, CH], BF16, name="fc_sb")
        U_sb = {}
        w_words = {}
        for x in GATES:
            U_sb[x] = keep.tile([P, CHUNKS, 2, CH], BF16, name="U_sb_" + x)
            w_words[x] = keep.tile([P, PASSES, 4 * CH], U8, name="w_words_" + x, align_bytes=64)

        U_chunks = {x: U_in[x].rearrange("(c p t) k -> c p t k", c=CHUNKS, t=2) for x in GATES}

        def load_U(x, c):
            nc.sync.dma_start(out=U_sb[x][:, c, :, :], in_=U_chunks[x][c])

        def load_bias(x, queue):
            queue.dma_start(out=bias_rows[x][0:1, :], in_=b_in[x].rearrange("(o n) -> o n", o=1))

        def load_scales(x, quadrant):
            nc.sync.dma_start(
                out=w_planes[32 * quadrant : 32 * quadrant + 4 * PASSES, column[x], :].bitcast(I32),
                in_=scales_in[x][:, 4 * quadrant : 4 * quadrant + 4, :].bitcast(I32),
            )

        def load_words(x):
            nc.sync.dma_start(
                out=w_words[x][:].bitcast(I32),
                in_=words_in[x].rearrange("g p n t -> p g (n t)").bitcast(I32),
            )

        def load_z(j):
            nc.sync.dma_start(out=z_sb[:, j, :], in_=z_rows[:, j, :])

        ht_rows = h_tilde.rearrange("(p j) k -> p j k", j=ROW_TILES)
        z_rows = z0.rearrange("(p j) k -> p j k", j=ROW_TILES)
        nc.sync.dma_start(out=ht_sb[:, 0, :], in_=ht_rows[:, 0, :])
        nc.scalar.activation(out=warm_out[:], in_=warm_in[:], func=SIGMOID)
        load_bias("o", nc.gpsimd)
        load_U("u", 0)
        load_bias("u", nc.sync)
        load_U("u", 1)
        nc.sync.dma_start(out=ht_sb[:, 1, :], in_=ht_rows[:, 1, :])
        load_bias("i", nc.sync)
        load_U("i", 0)
        load_scales("u", 0)
        load_U("i", 1)
        load_scales("u", 1)
        load_z(0)
        load_scales("u", 2)
        load_z(1)
        load_scales("u", 3)
        load_words("u")
        load_scales("i", 0)
        load_scales("i", 1)
        load_words("i")
        load_scales("i", 2)
        load_scales("i", 3)
        nc.sync.dma_start(out=U_sb["o"][:], in_=U_in["o"].rearrange("(c p t) k -> p c t k", c=CHUNKS, t=2))
        load_scales("o", 0)
        load_scales("o", 1)
        load_words("o")
        load_scales("o", 2)
        load_scales("o", 3)
        nc.sync.dma_start(out=fc_sb[:], in_=fc_sum.rearrange("(p j) k -> p j k", j=ROW_TILES))

        htT = keep.tile([P, ROW_TILES, HALVES, 2, P], BF16, name="htT")
        UT = {}
        for x in GATES:
            UT[x] = keep.tile([P, HALVES, 2 * CH], BF16, name="UT_" + x)
        bias_bc = keep.tile([P, 3, CH], BF16, name="bias_bc")
        z_sorted = keep.tile([P, ROW_TILES, SIZE], BF16, name="z_sorted")
        z_grouped = keep.tile([P, ROW_TILES, PASSES * P * 4], BF16, name="z_grouped", align_bytes=64)
        z_codes = keep.tile([P, ROW_TILES, PASSES * P], U32, name="z_codes", align_bytes=64)
        z_scales = keep.tile([P, ROW_TILES, PASSES * P], U8, name="z_scales", align_bytes=64)
        partial = {}
        gate = {}
        for j in range(ROW_TILES):
            for x in GATES:
                partial[(j, x)] = keep.tile([P, CH], F32, name="partial_%d_%s" % (j, x))
                gate[(j, x)] = keep.tile([P, CH], F32, name="gate_%d_%s" % (j, x))
        iu = [keep.tile([P, CH], F32, name="iu_%d" % j) for j in range(ROW_TILES)]
        tanh_c = [keep.tile([P, CH], F32, name="tanh_c_%d" % j) for j in range(ROW_TILES)]
        result = [keep.tile([P, 2 * CH], F32, name="result_%d" % j) for j in range(ROW_TILES)]
        out_rows = out.rearrange("(p j) n -> p j n", j=ROW_TILES)

        def new_bank():
            bank = psum.tile([P, BANK], F32, name="bank")
            return bank

        def warm_up():
            bank = new_bank()
            nc.tensor.matmul(
                out=bank[:, : WARM_ROUNDS * P].rearrange("p (r n) -> p r n", r=WARM_ROUNDS),
                lhsT=ones[:],
                rhs=ones[:].unsqueeze(1).to_broadcast([P, WARM_ROUNDS, P]),
                start=True,
                stop=True,
            )

        def transpose_ht(j, copy):
            bank = new_bank()
            ht_words = ht_sb[:].bitcast(F32)
            for u in range(HALVES):
                nc.tensor.transpose(
                    out=bank[:, u * P : (u + 1) * P],
                    in_=ht_words[:, j, u * P : (u + 1) * P],
                    identity=ident[:],
                )
            copy(
                out=htT[:, j, :, :, :],
                in_=bank[:, : HALVES * P].bitcast(BF16).rearrange("q (u p e) -> q u e p", u=HALVES, e=2),
            )

        def broadcast_bias(x):
            bank = new_bank()
            nc.tensor.matmul(out=bank[:], lhsT=ones_half[:], rhs=bias_rows[x][:], start=True, stop=True)
            return bank

        def keep_bias(x, bank):
            nc.scalar.copy(out=bias_bc[:, column[x], :], in_=bank[:])

        def transpose_U_halves(x, c, copies):
            U_words = U_sb[x][:].bitcast(F32)
            UT_words = UT[x][:].bitcast(F32)
            span = CH // CHUNKS
            for u in range(HALVES):
                bank = new_bank()
                for t in range(2):
                    nc.tensor.transpose(
                        out=bank[:, t * P : (t + 1) * P],
                        in_=U_words[:, c, t, u * P : (u + 1) * P],
                        identity=ident[:],
                    )
                copies[u](
                    out=UT_words[:, u, c * span : (c + 1) * span].rearrange("q (p t) -> q p t", t=2),
                    in_=bank[:, : 2 * P].rearrange("q (t p) -> q p t", t=2),
                )

        def transpose_U(x, c, copy):
            U_words = U_sb[x][:].bitcast(F32)
            UT_words = UT[x][:].bitcast(F32)
            span = CH // CHUNKS
            bank = new_bank()
            for t in range(2):
                for u in range(HALVES):
                    a = t * HALVES + u
                    nc.tensor.transpose(
                        out=bank[:, a * P : (a + 1) * P],
                        in_=U_words[:, c, t, u * P : (u + 1) * P],
                        identity=ident[:],
                    )
            copy(
                out=UT_words[:, :, c * span : (c + 1) * span].rearrange("q u (p t) -> q u p t", t=2),
                in_=bank[:].rearrange("q (t u p) -> q u p t", t=2, u=HALVES),
            )

        def sort_z(j):
            nc.vector.tensor_copy(
                out=z_sorted[:].bitcast(F32)[:, j, :].rearrange("p (u q) -> p u q", u=2),
                in_=z_sb[:].bitcast(F32)[:, j, :].rearrange("p (q u) -> p u q", u=2),
            )

        def transpose_z(j, copy):
            bank = new_bank()
            z_words = z_sorted[:].bitcast(F32)
            for a in range(2 * PASSES):
                nc.tensor.transpose(
                    out=bank[:, a * P : (a + 1) * P],
                    in_=z_words[:, j, a * P : (a + 1) * P],
                    identity=ident[:],
                )
            copy(
                out=z_grouped[:, j, :].bitcast(F32).rearrange("q (g b u) -> q g b u", g=PASSES, u=2),
                in_=bank[:].rearrange("q (u g b) -> q g b u", g=PASSES, u=2),
            )

        def quantise_z(j):
            nc.vector.quantize_mx(
                out=z_codes[:, j, :].bitcast(FP8X4), scales=z_scales[:, j, :], in_=z_grouped[:, j, :]
            )

        def plain_product(j, x, acc, cols):
            UT_pairs = UT[x][:].rearrange("q u (n e) -> q u n e", e=2)
            for u in range(HALVES):
                for e in range(2):
                    nc.tensor.matmul(
                        out=acc[:, cols],
                        lhsT=htT[:, j, u, e, :],
                        rhs=UT_pairs[:, u, cols, e],
                        start=(u == 0 and e == 0),
                        stop=(u == HALVES - 1 and e == 1),
                    )

        def mx_product(j, x):
            acc = new_bank()
            for g in range(PASSES):
                nc.tensor.matmul_mx(
                    out=acc[:],
                    lhsT=z_codes[:, j, g * P : (g + 1) * P].bitcast(FP8X4),
                    lhsT_scale=z_scales[:, j, g * P : (g + 1) * P],
                    rhs=w_words[x][:, g, :].bitcast(FP8X4),
                    rhs_scale=w_planes[4 * g : P, column[x], :],
                    start=(g == 0),
                    stop=(g == PASSES - 1),
                )
            return acc

        ALL = slice(0, CH)
        LEFT = slice(0, CH // 2)
        RIGHT = slice(CH // 2, CH)

        def add_bias(j, x, acc):
            nc.vector.tensor_tensor(out=partial[(j, x)][:], in0=acc[:], in1=bias_bc[:, column[x], :], op=ADD)

        def add_partial(j, x, acc, cols):
            nc.vector.tensor_tensor(
                out=partial[(j, x)][:, cols], in0=acc[:, cols], in1=partial[(j, x)][:, cols], op=ADD
            )

        def apply(j, x, cols):
            nc.scalar.activation(out=gate[(j, x)][:, cols], in_=partial[(j, x)][:, cols], func=func[x])

        def input_times_update(j, engine):
            engine.tensor_tensor(out=iu[j][:], in0=gate[(j, "i")][:], in1=gate[(j, "u")][:], op=MULT)

        def cell(j, engine):
            engine.tensor_tensor(out=result[j][:, CH:], in0=iu[j][:], in1=fc_sb[:, j, :], op=ADD)
            nc.sync.dma_start(out=out_rows[:, j, CH:], in_=result[j][:, CH:])

        def tanh_cell(j):
            nc.scalar.activation(out=tanh_c[j][:], in_=result[j][:, CH:], func=TANH)

        def hidden(j, cols):
            nc.vector.tensor_tensor(
                out=result[j][:, cols], in0=gate[(j, "o")][:, cols], in1=tanh_c[j][:, cols], op=MULT
            )
            nc.sync.dma_start(out=out_rows[:, j, cols], in_=result[j][:, cols])

        warm_up()
        transpose_ht(0, nc.vector.tensor_copy)
        transpose_U_halves("u", 0, (nc.scalar.copy, nc.vector.tensor_copy))
        bias_u = broadcast_bias("u")
        transpose_U_halves("u", 1, (nc.scalar.copy, nc.vector.tensor_copy))
        keep_bias("u", bias_u)
        transpose_ht(1, nc.scalar.copy)
        keep_bias("i", broadcast_bias("i"))
        acc = new_bank()
        plain_product(0, "u", acc, LEFT)
        plain_product(0, "u", acc, RIGHT)
        sort_z(0)
        add_bias(0, "u", acc)
        transpose_U("i", 0, nc.scalar.copy)
        transpose_U("i", 1, nc.vector.tensor_copy)
        sort_z(1)
        acc = new_bank()
        plain_product(1, "u", acc, ALL)
        add_bias(1, "u", acc)
        transpose_z(0, nc.scalar.copy)
        quantise_z(0)
        acc = new_bank()
        plain_product(0, "i", acc, ALL)
        add_bias(0, "i", acc)
        transpose_z(1, nc.scalar.copy)
        quantise_z(1)
        keep_bias("o", broadcast_bias("o"))
        for j, x in ((0, "u"), (0, "i"), (1, "u")):
            add_partial(j, x, mx_product(j, x), ALL)
            apply(j, x, ALL)
        input_times_update(0, nc.gpsimd)
        cell(0, nc.gpsimd)
        add_bias(1, "i", mx_product(1, "i"))
        acc = new_bank()
        plain_product(1, "i", acc, ALL)
        add_partial(1, "i", acc, ALL)
        transpose_U("o", 0, nc.scalar.copy)
        apply(1, "i", ALL)
        transpose_U("o", 1, nc.vector.tensor_copy)
        tanh_cell(0)
        for j in range(ROW_TILES):
            add_bias(j, "o", mx_product(j, "o"))
        input_times_update(1, nc.vector)
        acc = new_bank()
        plain_product(0, "o", acc, ALL)
        add_partial(0, "o", acc, ALL)
        apply(0, "o", ALL)
        cell(1, nc.vector)
        tanh_cell(1)
        acc = new_bank()
        plain_product(1, "o", acc, LEFT)
        add_partial(1, "o", acc, LEFT)
        apply(1, "o", LEFT)
        acc = new_bank()
        plain_product(1, "o", acc, RIGHT)
        add_partial(1, "o", acc, RIGHT)
        apply(1, "o", RIGHT)
        hidden(0, ALL)
        hidden(1, LEFT)
        hidden(1, RIGHT)
